import numpy as np
import ml_dtypes


def mxq(x, axis, fmt="e4m3"):
    dtype, down = {"e4m3": (ml_dtypes.float8_e4m3fn, 7), "e5m2": (ml_dtypes.float8_e5m2, 14)}[fmt]
    v = np.moveaxis(np.asarray(x, np.float32).astype(ml_dtypes.bfloat16).astype(np.float64), axis, -1)
    blocks = v.reshape(v.shape[:-1] + (-1, 32))
    amax = np.abs(blocks).max(-1, keepdims=True)
    byte = np.maximum(np.where(amax > 0, np.frexp(amax)[1] - 1 + 127, 0) - down, 1)
    scale = np.exp2(byte - 127.0)
    codes = (blocks / scale).astype(np.float32).astype(dtype).astype(np.float64)
    return np.moveaxis((codes * scale).reshape(v.shape), -1, axis)


WIDE = False


def mx_kscale(k):
    if not WIDE:
        return np.ones(k)
    levels = np.array([10, -10, 5, -5, 0])
    a = np.random.permutation(np.resize(levels, k // 512 * 4)).reshape(k // 512, 4)
    idx = np.arange(k)
    return np.exp2(a[idx // 512, idx % 128 // 32])


BF16 = ml_dtypes.bfloat16


def bf(x):
    return np.asarray(x, np.float32).astype(BF16)


def f64(x):
    return np.asarray(x).astype(np.float64)


N, DI, DO, M = 16, 1024, 256, 8
NB = 19


def mix(cb, tq):
    rest = tq.shape[2:]
    y = cb.T @ np.moveaxis(tq, 1, 0).reshape(DI, -1)
    return np.moveaxis(y.reshape((DO, N) + rest), 0, 1)


def setup_inputs():
    s = mx_kscale(DI)
    g = np.concatenate([np.ones(1), np.full(9, 1.0 / np.sqrt(M)), np.full(9, 1.0 / M)])
    return {"x": bf(np.random.standard_normal((N, DI, M, M, M)) * s[None, :, None, None, None]),
            "coefs": bf(np.random.standard_normal((DI, DO, NB)) * (0.5 / np.sqrt(DI)) * g / s[:, None, None]),
            "bias": bf(np.random.standard_normal((1, DO, 1, 1, 1)) * 0.5)}


def reference(x, coefs, bias):
    x = f64(x)
    cq = mxq(f64(coefs), 0, "e4m3")
    out = mix(cq[:, :, 0], mxq(x, 1, "e4m3"))
    b = 1
    for ax in (2, 3, 4):
        mq = mxq(x.sum(axis=ax), 1, "e4m3")
        for pos in (2, 3, 4):
            out = out + np.expand_dims(mix(cq[:, :, b], mq), pos)
            b += 1
    for axes in ((2, 3), (2, 4), (3, 4)):
        vq = mxq(x.sum(axis=axes), 1, "e4m3")
        for pos in (2, 3, 4):
            shape = [N, DO, 1, 1, 1]
            shape[pos] = M
            out = out + mix(cq[:, :, b], vq).reshape(shape)
            b += 1
    return out + f64(bias)

@@ -1,0 +1,292 @@
+from contextlib import ExitStack
+
+import concourse.mybir as mybir
+from concourse.masks import make_identity
+
+F32 = mybir.dt.float32
+BF16 = mybir.dt.bfloat16
+U32 = mybir.dt.uint32
+U8 = mybir.dt.uint8
+FP8X4 = mybir.dt.float8_e4m3fn_x4
+ADD = mybir.AluOpType.add
+MULT = mybir.AluOpType.mult
+AX = mybir.AxisListType.X
+AXY = mybir.AxisListType.XY
+IDENT = mybir.ActivationFunctionType.Identity
+
+P = 128
+NBATCH = 16
+GN = 4
+NB = 19
+FLOPS = 2 * 1024 * 256 * (8192 + 9 * 1024 + 9 * 128)
+
+
+def tile_seteq3to3_t_kernel(tc, x, coefs, bias, out):
+    nc = tc.nc
+    x_v = x.rearrange("n (g p t) i j k -> n p g (t i j k)", g=2, p=P, t=4)
+    c_v = coefs.rearrange("(g p t) s b -> g p t (s b)", g=2, p=P, t=4)
+    o_v = out.rearrange("n (m p) i j k -> n p m (i j k)", m=2, p=P)
+    b_v = bias.rearrange("o (m p) a b c -> (o m) (p a b c)", m=2, p=P)
+
+    with ExitStack() as ctx:
+        keep = ctx.enter_context(tc.tile_pool(name="keep", bufs=1))
+        xin = ctx.enter_context(tc.tile_pool(name="xin", bufs=3))
+        xtp = ctx.enter_context(tc.tile_pool(name="xtp", bufs=2))
+        xgp = ctx.enter_context(tc.tile_pool(name="xgp", bufs=2))
+        xcd = ctx.enter_context(tc.tile_pool(name="xcd", bufs=7))
+        agp = ctx.enter_context(tc.tile_pool(name="agp", bufs=2))
+        pst = ctx.enter_context(tc.psum_pool(name="pst", bufs=2))
+        psa = ctx.enter_context(tc.psum_pool(name="psa", bufs=2))
+        psv = ctx.enter_context(tc.psum_pool(name="psv", bufs=1))
+        psm = ctx.enter_context(tc.psum_pool(name="psm", bufs=2))
+        psq = ctx.enter_context(tc.psum_pool(name="psq", bufs=1))
+
+        cq = keep.tile([P, 4 * NB * P], U32, align_bytes=64, name="cq")
+        cs = keep.tile([P, 4 * NB * P], U8, align_bytes=64, name="cs")
+
+        raws = {}
+
+        def load(n):
+            raw = xin.tile([P, 4096], BF16, name="raw")
+            nc.sync.dma_start(out=raw[:].rearrange("p (g w) -> p g w", g=2), in_=x_v[n])
+            raws[n] = raw
+
+        load(0)
+        load(1)
+
+        ident = keep.tile([P, P], BF16, name="ident")
+        make_identity(nc, ident[:])
+
+        sf = keep.tile([P, P], F32, name="sf")
+        nc.vector.memset(sf[:], 0.0)
+        nc.vector.tensor_reduce(
+            out=sf[:, 0:16].rearrange("p (i k) -> p i k", i=2),
+            in_=ident[:].rearrange("p (i j k) -> p i k j", i=2, j=8), axis=AX, op=ADD,
+        )
+        nc.vector.tensor_reduce(out=sf[:, 16:32], in_=ident[:].rearrange("p (e k) -> p e k", k=8), axis=AX, op=ADD)
+        for c in range(4):
+            o = 32 + 24 * c
+            nc.vector.tensor_reduce(out=sf[:, o : o + 8], in_=ident[:].rearrange("p (e k) -> p k e", k=8), axis=AX, op=ADD)
+            nc.vector.tensor_reduce(
+                out=sf[:, o + 8 : o + 16], in_=ident[:].rearrange("p (i j k) -> p j i k", i=2, j=8), axis=AXY, op=ADD
+            )
+            nc.vector.tensor_reduce(
+                out=sf[:, o + 16 + 2 * c : o + 18 + 2 * c], in_=ident[:].rearrange("p (i e) -> p i e", i=2), axis=AX, op=ADD
+            )
+        sb = keep.tile([P, P], BF16, name="sb")
+        nc.vector.tensor_copy(out=sb[:], in_=sf[:])
+
+        bz = keep.tile([P, P], BF16, name="bz")
+        nc.vector.memset(bz[:], 0.0)
+        nc.sync.dma_start(out=bz[0:2, :], in_=b_v)
+        bps = pst.tile([P, 1024], BF16, name="bps", tag="tp")
+        nc.tensor.transpose(bps[:, 0:P], bz[:], ident[:])
+        bias_sb = keep.tile([P, 2], F32, name="bias_sb")
+        nc.vector.tensor_copy(out=bias_sb[:], in_=bps[:, 0:2])
+
+        vgrs = []
+        for h in range(2):
+            vgr = keep.tile([P, 3072], BF16, align_bytes=64, name="vgr%d" % h)
+            nc.vector.memset(vgr[:], 0.0)
+            vgrs.append(vgr)
+
+        agrs = {}
+        xqs = {}
+
+        def front(n):
+            grp, ni = divmod(n, GN)
+            if n + 2 < NBATCH:
+                load(n + 2)
+            raw = raws[n]
+            if ni == 0:
+                agrs[grp] = agp.tile([P, 3 * 2048], BF16, align_bytes=64, name="agr")
+            agr_v = agrs[grp][:].rearrange("p (a g n q t) -> p a g n q t", a=3, g=2, n=GN, t=4)
+            vgr_v = vgrs[grp % 2][:].rearrange("p (v g c t) -> p v g c t", v=3, g=2, t=4)
+            xT = xtp.tile([P, 4096], BF16, name="xT")
+            for u in range(4):
+                tp = pst.tile([P, 1024], BF16, name="tp")
+                for r in range(8):
+                    o = (u * 8 + r) * P
+                    nc.tensor.transpose(tp[:, r * P : (r + 1) * P], raw[:, o : o + P], ident[:])
+                nc.scalar.copy(out=xT[:, u * 1024 : (u + 1) * 1024], in_=tp[:])
+            with nc.allow_low_precision(reason="the sum is made in float32 and rounded once to bfloat16"):
+                for g in range(2):
+                    nc.vector.tensor_reduce(
+                        out=agr_v[:, 0, g, ni],
+                        in_=raw[:, g * 2048 : (g + 1) * 2048].rearrange("p (t i q) -> p q t i", t=4, i=8),
+                        axis=AX, op=ADD,
+                    )
+            sv = psv.tile([P, 512], F32, name="sv")
+            for g in range(2):
+                sa = psa.tile([P, 512], F32, name="sa")
+                for t in range(4):
+                    for c in range(4):
+                        o = ((g * 4 + t) * 4 + c) * P
+                        nc.tensor.matmul(
+                            out=sa[:, (t * 4 + c) * 32 : (t * 4 + c + 1) * 32],
+                            lhsT=xT[:, o : o + P], rhs=sb[:, 0:32], start=True, stop=True,
+                        )
+                        nc.tensor.matmul(
+                            out=sv[:, (g * 4 + t) * 24 : (g * 4 + t + 1) * 24],
+                            lhsT=xT[:, o : o + P], rhs=sb[:, 32 + 24 * c : 56 + 24 * c], start=(c == 0), stop=(c == 3),
+                        )
+                sa_v = sa[:].rearrange("p (t c a e) -> p a c e t", t=4, c=4, a=2)
+                for a in range(2):
+                    nc.scalar.copy(
+                        out=agr_v[:, 1 + a, g, ni].rearrange("p (c e) t -> p c e t", c=4), in_=sa_v[:, a]
+                    )
+                nc.scalar.copy(
+                    out=vgr_v[:, :, g, ni * 8 : (ni + 1) * 8, :],
+                    in_=sv[:, g * 96 : (g + 1) * 96].rearrange("p (t v r) -> p v r t", t=4, v=3),
+                )
+            xq = xcd.tile([P, 1024], U32, align_bytes=64, name="xq")
+            xs = xcd.tile([P, 1024], U8, align_bytes=64, name="xs")
+            xgs = []
+            for g in range(2):
+                xg = xgp.tile([P, 2048], BF16, align_bytes=64, name="xg%d" % g)
+                dst = xg[:].rearrange("p (c i t) -> p c t i", i=4, t=4)
+                src = raw[:, g * 2048 : (g + 1) * 2048].rearrange("p (t c i) -> p c t i", t=4, i=4)
+                if g == 0:
+                    nc.vector.tensor_copy(out=dst, in_=src)
+                else:
+                    nc.scalar.copy(out=dst, in_=src)
+                xgs.append(xg)
+            for g in range(2):
+                nc.vector.quantize_mx(
+                    out=xq[:, g * 512 : (g + 1) * 512].bitcast(FP8X4), scales=xs[:, g * 512 : (g + 1) * 512], in_=xgs[g][:]
+                )
+            xqs[n] = (xq, xs)
+
+        with tc.tile_pool(name="cst", bufs=2) as cst:
+            for step in range(4):
+                m, g = divmod(step, 2)
+                craw = cst.tile([P, 4, 128 * NB], BF16, name="craw")
+                nc.gpsimd.dma_start(out=craw[:], in_=c_v[g][:, :, m * 128 * NB : (m + 1) * 128 * NB])
+                front(step)
+                src = craw[:].rearrange("p t (s b) -> p b s t", b=NB)
+                base = (g * 2 + m) * NB * P
+                for b0, b1, who in ((0, 8, "s"), (8, 16, "g"), (16, 19, "v")):
+                    cgr = cst.tile([P, 4096], BF16, align_bytes=64, name="cgr")
+                    dst = cgr[:, 0 : (b1 - b0) * 512].rearrange("p (b s t) -> p b s t", b=b1 - b0, t=4)
+                    if who == "s":
+                        nc.scalar.copy(out=dst, in_=src[:, b0:b1])
+                    elif who == "g":
+                        nc.gpsimd.tensor_scalar(out=dst, in0=src[:, b0:b1], scalar1=1.0, scalar2=0.0, op0=MULT, op1=ADD)
+                    else:
+                        nc.vector.tensor_copy(out=dst, in_=src[:, b0:b1])
+                    pieces = ((0, 8),) if b1 - b0 == 8 else ((0, 2), (2, 3))
+                    for q0, q1 in pieces:
+                        nc.vector.quantize_mx(
+                            out=cq[:, base + (b0 + q0) * P : base + (b0 + q1) * P].bitcast(FP8X4),
+                            scales=cs[:, base + (b0 + q0) * P : base + (b0 + q1) * P],
+                            in_=cgr[:, q0 * 512 : q1 * 512],
+                        )
+
+        def cw(g, m, b):
+            o = ((g * 2 + m) * NB + b) * P
+            return cq[:, o : o + P].bitcast(FP8X4), cs[:, o : o + P]
+
+        late = ctx.enter_context(tc.tile_pool(name="late", bufs=2))
+        psbs = {}
+
+        def group_stage(grp):
+            agr = agrs[grp]
+            vgr = vgrs[grp % 2]
+            aq = late.tile([P, 1536], U32, align_bytes=64, name="aq")
+            asc = late.tile([P, 1536], U8, align_bytes=64, name="asc")
+            vq = late.tile([P, 768], U32, align_bytes=64, name="vq")
+            vs = late.tile([P, 768], U8, align_bytes=64, name="vs")
+            nc.vector.quantize_mx(out=vq[:, 0:512].bitcast(FP8X4), scales=vs[:, 0:512], in_=vgr[:, 0:2048])
+            nc.vector.quantize_mx(out=vq[:, 512:768].bitcast(FP8X4), scales=vs[:, 512:768], in_=vgr[:, 2048:3072])
+            for a3 in range(3):
+                nc.vector.quantize_mx(
+                    out=aq[:, a3 * 512 : (a3 + 1) * 512].bitcast(FP8X4),
+                    scales=asc[:, a3 * 512 : (a3 + 1) * 512],
+                    in_=agr[:, a3 * 2048 : (a3 + 1) * 2048],
+                )
+            for m in range(2):
+                qsb = late.tile([P, 3, GN * 8], F32, name="qsb%d" % m)
+                for pl in range(3):
+                    qps = psq.tile([P, 512], F32, name="qps", tag="pq")
+                    for idx in range(6):
+                        a3, g = divmod(idx, 2)
+                        w, wsc = cw(g, m, 10 + 3 * a3 + pl)
+                        o = (a3 * 2 + g) * P
+                        nc.tensor.matmul_mx(
+                            out=qps[:, 0:P], lhsT=w, lhsT_scale=wsc,
+                            rhs=vq[:, o : o + P].bitcast(FP8X4), rhs_scale=vs[:, o : o + P],
+                            start=(idx == 0), stop=(idx == 5),
+                        )
+                    if pl == 0:
+                        nc.scalar.activation(out=qsb[:, 0], in_=qps[:, 0 : GN * 8], func=IDENT, bias=bias_sb[:, m : m + 1])
+                    else:
+                        nc.scalar.copy(out=qsb[:, pl], in_=qps[:, 0 : GN * 8])
+                psb = late.tile([P, 3, GN * 64], F32, name="psb%d" % m)
+                for pl in range(3):
+                    pps = psq.tile([P, 512], F32, name="pps", tag="pq")
+                    for idx in range(6):
+                        a3, g = divmod(idx, 2)
+                        w, wsc = cw(g, m, 1 + 3 * a3 + pl)
+                        o = a3 * 512 + g * 256
+                        nc.tensor.matmul_mx(
+                            out=pps[:, 0:256], lhsT=w, lhsT_scale=wsc,
+                            rhs=aq[:, o : o + 256].bitcast(FP8X4), rhs_scale=asc[:, o : o + 256],
+                            start=(idx == 0), stop=(idx == 5),
+                        )
+                    if pl == 2:
+                        nc.scalar.copy(out=psb[:, 2], in_=pps[:, 0:256])
+                    else:
+                        nc.vector.tensor_tensor(
+                            out=psb[:, pl].rearrange("p (e k) -> p e k", k=8),
+                            in0=pps[:, 0:256].rearrange("p (e k) -> p e k", k=8),
+                            in1=qsb[:, 1 - pl].unsqueeze(2).to_broadcast([P, GN * 8, 8]),
+                            op=ADD,
+                        )
+                nc.vector.tensor_tensor(
+                    out=psb[:, 0].rearrange("p (n j k) -> p n j k", n=GN, k=8),
+                    in0=psb[:, 0].rearrange("p (n j k) -> p n j k", n=GN, k=8),
+                    in1=qsb[:, 2].rearrange("p (n k) -> p n k", n=GN).unsqueeze(2).to_broadcast([P, GN, 8, 8]),
+                    op=ADD,
+                )
+                psbs[(grp, m)] = psb
+
+        def back(n):
+            grp, ni = divmod(n, GN)
+            xq, xs = xqs[n]
+            osb = late.tile([P, 2, 512], F32, name="osb")
+            sl = slice(ni * 64, (ni + 1) * 64)
+            for m in range(2):
+                psb = psbs[(grp, m)]
+                b1 = late.tile([P, 512], F32, name="b1")
+                nc.gpsimd.tensor_tensor(
+                    out=b1[:].rearrange("p (i j k) -> p i j k", i=8, j=8),
+                    in0=psb[:, 0, sl].rearrange("p (j k) -> p j k", j=8).unsqueeze(1).to_broadcast([P, 8, 8, 8]),
+                    in1=psb[:, 1, sl].rearrange("p (i k) -> p i k", i=8).unsqueeze(2).to_broadcast([P, 8, 8, 8]),
+                    op=ADD,
+                )
+                b2 = late.tile([P, 512], F32, name="b2")
+                nc.gpsimd.tensor_tensor(
+                    out=b2[:].rearrange("p (e k) -> p e k", k=8),
+                    in0=b1[:].rearrange("p (e k) -> p e k", k=8),
+                    in1=psb[:, 2, sl].unsqueeze(2).to_broadcast([P, 64, 8]),
+                    op=ADD,
+                )
+                mps = psm.tile([P, 512], F32, name="mps")
+                for g in range(2):
+                    w, wsc = cw(g, m, 0)
+                    nc.tensor.matmul_mx(
+                        out=mps[:], lhsT=w, lhsT_scale=wsc,
+                        rhs=xq[:, g * 512 : (g + 1) * 512].bitcast(FP8X4), rhs_scale=xs[:, g * 512 : (g + 1) * 512],
+                        start=(g == 0), stop=(g == 1),
+                    )
+                nc.vector.tensor_tensor(out=osb[:, m], in0=mps[:], in1=b2[:], op=ADD)
+            nc.sync.dma_start(out=o_v[n], in_=osb[:])
+
+        group_stage(0)
+        for n in range(GN, NBATCH):
+            front(n)
+            back(n - GN)
+            if n % GN == GN - 1:
+                group_stage(n // GN)
+        for n in range(NBATCH - GN, NBATCH):
+            back(n)

@@ -16,7 +16,7 @@ IDENT = mybir.ActivationFunctionType.Identity
 
 P = 128
 NBATCH = 16
-GN = 4
+GROUPS = ((0, 4), (4, 4), (8, 4), (12, 2), (14, 2))
 NB = 19
 FLOPS = 2 * 1024 * 256 * (8192 + 9 * 1024 + 9 * 128)
 
@@ -33,13 +33,13 @@ def tile_seteq3to3_t_kernel(tc, x, coefs, bias, out):
         xin = ctx.enter_context(tc.tile_pool(name="xin", bufs=3))
         xtp = ctx.enter_context(tc.tile_pool(name="xtp", bufs=2))
         xgp = ctx.enter_context(tc.tile_pool(name="xgp", bufs=2))
-        xcd = ctx.enter_context(tc.tile_pool(name="xcd", bufs=7))
+        xcd = ctx.enter_context(tc.tile_pool(name="xcd", bufs=6))
+        s1p = ctx.enter_context(tc.tile_pool(name="s1p", bufs=2))
         agp = ctx.enter_context(tc.tile_pool(name="agp", bufs=2))
         pst = ctx.enter_context(tc.psum_pool(name="pst", bufs=2))
         psa = ctx.enter_context(tc.psum_pool(name="psa", bufs=2))
         psv = ctx.enter_context(tc.psum_pool(name="psv", bufs=1))
-        psm = ctx.enter_context(tc.psum_pool(name="psm", bufs=2))
-        psq = ctx.enter_context(tc.psum_pool(name="psq", bufs=1))
+        psx = ctx.enter_context(tc.psum_pool(name="psx", bufs=3))
 
         cq = keep.tile([P, 4 * NB * P], U32, align_bytes=64, name="cq")
         cs = keep.tile([P, 4 * NB * P], U8, align_bytes=64, name="cs")
@@ -91,16 +91,32 @@ def tile_seteq3to3_t_kernel(tc, x, coefs, bias, out):
             vgrs.append(vgr)
 
         agrs = {}
+        group_of = {}
+        for gi, (n0, gn) in enumerate(GROUPS):
+            for n in range(n0, n0 + gn):
+                group_of[n] = gi
         xqs = {}
 
         def front(n):
-            grp, ni = divmod(n, GN)
+            grp = group_of[n]
+            n0, gn = GROUPS[grp]
+            ni = n - n0
             if n + 2 < NBATCH:
                 load(n + 2)
             raw = raws[n]
             if ni == 0:
-                agrs[grp] = agp.tile([P, 3 * 2048], BF16, align_bytes=64, name="agr")
-            agr_v = agrs[grp][:].rearrange("p (a g n q t) -> p a g n q t", a=3, g=2, n=GN, t=4)
+                agrs[grp] = agp.tile([P, 3, 2048], BF16, align_bytes=64, name="agr")
+            agr_v = agrs[grp][:, :, 0 : gn * 512].rearrange("p a (g n q t) -> p a g n q t", g=2, n=gn, t=4)
+            xgs = []
+            for g in range(2):
+                xg = xgp.tile([P, 2048], BF16, align_bytes=64, name="xg%d" % g)
+                dst = xg[:].rearrange("p (c i t) -> p c t i", i=4, t=4)
+                src = raw[:, g * 2048 : (g + 1) * 2048].rearrange("p (t c i) -> p c t i", t=4, i=4)
+                if g == 0:
+                    nc.vector.tensor_copy(out=dst, in_=src)
+                else:
+                    nc.scalar.copy(out=dst, in_=src)
+                xgs.append(xg)
             vgr_v = vgrs[grp % 2][:].rearrange("p (v g c t) -> p v g c t", v=3, g=2, t=4)
             xT = xtp.tile([P, 4096], BF16, name="xT")
             for u in range(4):
@@ -109,13 +125,14 @@ def tile_seteq3to3_t_kernel(tc, x, coefs, bias, out):
                     o = (u * 8 + r) * P
                     nc.tensor.transpose(tp[:, r * P : (r + 1) * P], raw[:, o : o + P], ident[:])
                 nc.scalar.copy(out=xT[:, u * 1024 : (u + 1) * 1024], in_=tp[:])
-            with nc.allow_low_precision(reason="the sum is made in float32 and rounded once to bfloat16"):
-                for g in range(2):
-                    nc.vector.tensor_reduce(
-                        out=agr_v[:, 0, g, ni],
-                        in_=raw[:, g * 2048 : (g + 1) * 2048].rearrange("p (t i q) -> p q t i", t=4, i=8),
-                        axis=AX, op=ADD,
-                    )
+            s1 = s1p.tile([P, 2, 2, 256], F32, name="s1")
+            for g in range(2):
+                nc.vector.tensor_reduce(
+                    out=s1[:, g], in_=xgs[g][:].rearrange("p (h i e) -> p h e i", h=2, i=4), axis=AX, op=ADD
+                )
+            nc.vector.tensor_tensor(
+                out=agr_v[:, 0, :, ni].rearrange("p g q t -> p g (q t)"), in0=s1[:, :, 0], in1=s1[:, :, 1], op=ADD
+            )
             sv = psv.tile([P, 512], F32, name="sv")
             for g in range(2):
                 sa = psa.tile([P, 512], F32, name="sa")
@@ -141,16 +158,6 @@ def tile_seteq3to3_t_kernel(tc, x, coefs, bias, out):
                 )
             xq = xcd.tile([P, 1024], U32, align_bytes=64, name="xq")
             xs = xcd.tile([P, 1024], U8, align_bytes=64, name="xs")
-            xgs = []
-            for g in range(2):
-                xg = xgp.tile([P, 2048], BF16, align_bytes=64, name="xg%d" % g)
-                dst = xg[:].rearrange("p (c i t) -> p c t i", i=4, t=4)
-                src = raw[:, g * 2048 : (g + 1) * 2048].rearrange("p (t c i) -> p c t i", t=4, i=4)
-                if g == 0:
-                    nc.vector.tensor_copy(out=dst, in_=src)
-                else:
-                    nc.scalar.copy(out=dst, in_=src)
-                xgs.append(xg)
             for g in range(2):
                 nc.vector.quantize_mx(
                     out=xq[:, g * 512 : (g + 1) * 512].bitcast(FP8X4), scales=xs[:, g * 512 : (g + 1) * 512], in_=xgs[g][:]
@@ -190,6 +197,7 @@ def tile_seteq3to3_t_kernel(tc, x, coefs, bias, out):
         psbs = {}
 
         def group_stage(grp):
+            gn = GROUPS[grp][1]
             agr = agrs[grp]
             vgr = vgrs[grp % 2]
             aq = late.tile([P, 1536], U32, align_bytes=64, name="aq")
@@ -200,14 +208,14 @@ def tile_seteq3to3_t_kernel(tc, x, coefs, bias, out):
             nc.vector.quantize_mx(out=vq[:, 512:768].bitcast(FP8X4), scales=vs[:, 512:768], in_=vgr[:, 2048:3072])
             for a3 in range(3):
                 nc.vector.quantize_mx(
-                    out=aq[:, a3 * 512 : (a3 + 1) * 512].bitcast(FP8X4),
-                    scales=asc[:, a3 * 512 : (a3 + 1) * 512],
-                    in_=agr[:, a3 * 2048 : (a3 + 1) * 2048],
+                    out=aq[:, a3 * 512 : a3 * 512 + gn * 128].bitcast(FP8X4),
+                    scales=asc[:, a3 * 512 : a3 * 512 + gn * 128],
+                    in_=agr[:, a3, 0 : gn * 512],
                 )
             for m in range(2):
-                qsb = late.tile([P, 3, GN * 8], F32, name="qsb%d" % m)
+                qsb = late.tile([P, 3, 32], F32, name="qsb%d" % m)
                 for pl in range(3):
-                    qps = psq.tile([P, 512], F32, name="qps", tag="pq")
+                    qps = psx.tile([P, 512], F32, name="qps", tag="mx")
                     for idx in range(6):
                         a3, g = divmod(idx, 2)
                         w, wsc = cw(g, m, 10 + 3 * a3 + pl)
@@ -218,60 +226,60 @@ def tile_seteq3to3_t_kernel(tc, x, coefs, bias, out):
                             start=(idx == 0), stop=(idx == 5),
                         )
                     if pl == 0:
-                        nc.scalar.activation(out=qsb[:, 0], in_=qps[:, 0 : GN * 8], func=IDENT, bias=bias_sb[:, m : m + 1])
+                        nc.scalar.activation(out=qsb[:, 0, 0 : gn * 8], in_=qps[:, 0 : gn * 8], func=IDENT, bias=bias_sb[:, m : m + 1])
                     else:
-                        nc.scalar.copy(out=qsb[:, pl], in_=qps[:, 0 : GN * 8])
-                psb = late.tile([P, 3, GN * 64], F32, name="psb%d" % m)
+                        nc.scalar.copy(out=qsb[:, pl, 0 : gn * 8], in_=qps[:, 0 : gn * 8])
+                psb = late.tile([P, 3, 256], F32, name="psb%d" % m)
+                nw = gn * 64
                 for pl in range(3):
-                    pps = psq.tile([P, 512], F32, name="pps", tag="pq")
+                    pps = psx.tile([P, 512], F32, name="pps", tag="mx")
                     for idx in range(6):
                         a3, g = divmod(idx, 2)
                         w, wsc = cw(g, m, 1 + 3 * a3 + pl)
-                        o = a3 * 512 + g * 256
+                        o = a3 * 512 + g * nw
                         nc.tensor.matmul_mx(
-                            out=pps[:, 0:256], lhsT=w, lhsT_scale=wsc,
-                            rhs=aq[:, o : o + 256].bitcast(FP8X4), rhs_scale=asc[:, o : o + 256],
+                            out=pps[:, 0:nw], lhsT=w, lhsT_scale=wsc,
+                            rhs=aq[:, o : o + nw].bitcast(FP8X4), rhs_scale=asc[:, o : o + nw],
                             start=(idx == 0), stop=(idx == 5),
                         )
                     if pl == 2:
-                        nc.scalar.copy(out=psb[:, 2], in_=pps[:, 0:256])
+                        nc.scalar.copy(out=psb[:, 2, 0:nw], in_=pps[:, 0:nw])
                     else:
                         nc.vector.tensor_tensor(
-                            out=psb[:, pl].rearrange("p (e k) -> p e k", k=8),
-                            in0=pps[:, 0:256].rearrange("p (e k) -> p e k", k=8),
-                            in1=qsb[:, 1 - pl].unsqueeze(2).to_broadcast([P, GN * 8, 8]),
+                            out=psb[:, pl, 0:nw].rearrange("p (e k) -> p e k", k=8),
+                            in0=pps[:, 0:nw].rearrange("p (e k) -> p e k", k=8),
+                            in1=qsb[:, 1 - pl, 0 : gn * 8].unsqueeze(2).to_broadcast([P, gn * 8, 8]),
                             op=ADD,
                         )
                 nc.vector.tensor_tensor(
-                    out=psb[:, 0].rearrange("p (n j k) -> p n j k", n=GN, k=8),
-                    in0=psb[:, 0].rearrange("p (n j k) -> p n j k", n=GN, k=8),
-                    in1=qsb[:, 2].rearrange("p (n k) -> p n k", n=GN).unsqueeze(2).to_broadcast([P, GN, 8, 8]),
+                    out=psb[:, 0, 0:nw].rearrange("p (n j k) -> p n j k", n=gn, k=8),
+                    in0=psb[:, 0, 0:nw].rearrange("p (n j k) -> p n j k", n=gn, k=8),
+                    in1=qsb[:, 2, 0 : gn * 8].rearrange("p (n k) -> p n k", n=gn).unsqueeze(2).to_broadcast([P, gn, 8, 8]),
                     op=ADD,
                 )
                 psbs[(grp, m)] = psb
 
         def back(n):
-            grp, ni = divmod(n, GN)
+            grp = group_of[n]
+            ni = n - GROUPS[grp][0]
+            last = grp == len(GROUPS) - 1
             xq, xs = xqs[n]
             osb = late.tile([P, 2, 512], F32, name="osb")
             sl = slice(ni * 64, (ni + 1) * 64)
             for m in range(2):
                 psb = psbs[(grp, m)]
+                p0b = psb[:, 0, sl].rearrange("p (j k) -> p j k", j=8).unsqueeze(1).to_broadcast([P, 8, 8, 8])
+                p1b = psb[:, 1, sl].rearrange("p (i k) -> p i k", i=8).unsqueeze(2).to_broadcast([P, 8, 8, 8])
+                p2b = psb[:, 2, sl].unsqueeze(2).to_broadcast([P, 64, 8])
                 b1 = late.tile([P, 512], F32, name="b1")
-                nc.gpsimd.tensor_tensor(
-                    out=b1[:].rearrange("p (i j k) -> p i j k", i=8, j=8),
-                    in0=psb[:, 0, sl].rearrange("p (j k) -> p j k", j=8).unsqueeze(1).to_broadcast([P, 8, 8, 8]),
-                    in1=psb[:, 1, sl].rearrange("p (i k) -> p i k", i=8).unsqueeze(2).to_broadcast([P, 8, 8, 8]),
-                    op=ADD,
-                )
                 b2 = late.tile([P, 512], F32, name="b2")
-                nc.gpsimd.tensor_tensor(
-                    out=b2[:].rearrange("p (e k) -> p e k", k=8),
-                    in0=b1[:].rearrange("p (e k) -> p e k", k=8),
-                    in1=psb[:, 2, sl].unsqueeze(2).to_broadcast([P, 64, 8]),
-                    op=ADD,
-                )
-                mps = psm.tile([P, 512], F32, name="mps")
+                on_vector = last and m == 1
+                if not on_vector:
+                    nc.gpsimd.tensor_tensor(out=b1[:].rearrange("p (i j k) -> p i j k", i=8, j=8), in0=p0b, in1=p1b, op=ADD)
+                    nc.gpsimd.tensor_tensor(
+                        out=b2[:].rearrange("p (e k) -> p e k", k=8), in0=b1[:].rearrange("p (e k) -> p e k", k=8), in1=p2b, op=ADD
+                    )
+                mps = psx.tile([P, 512], F32, name="mps", tag="mx")
                 for g in range(2):
                     w, wsc = cw(g, m, 0)
                     nc.tensor.matmul_mx(
@@ -279,14 +287,33 @@ def tile_seteq3to3_t_kernel(tc, x, coefs, bias, out):
                         rhs=xq[:, g * 512 : (g + 1) * 512].bitcast(FP8X4), rhs_scale=xs[:, g * 512 : (g + 1) * 512],
                         start=(g == 0), stop=(g == 1),
                     )
-                nc.vector.tensor_tensor(out=osb[:, m], in0=mps[:], in1=b2[:], op=ADD)
+                if on_vector:
+                    nc.vector.tensor_tensor(
+                        out=b1[:].rearrange("p (i j k) -> p i j k", i=8, j=8),
+                        in0=mps[:].rearrange("p (i j k) -> p i j k", i=8, j=8), in1=p0b, op=ADD,
+                    )
+                    nc.vector.tensor_tensor(
+                        out=b2[:].rearrange("p (i j k) -> p i j k", i=8, j=8),
+                        in0=b1[:].rearrange("p (i j k) -> p i j k", i=8, j=8), in1=p1b, op=ADD,
+                    )
+                    nc.vector.tensor_tensor(
+                        out=osb[:, m].rearrange("p (e k) -> p e k", k=8), in0=b2[:].rearrange("p (e k) -> p e k", k=8), in1=p2b, op=ADD
+                    )
+                else:
+                    nc.vector.tensor_tensor(out=osb[:, m], in0=mps[:], in1=b2[:], op=ADD)
             nc.sync.dma_start(out=o_v[n], in_=osb[:])
 
         group_stage(0)
-        for n in range(GN, NBATCH):
+        ready = 4
+        done = 0
+        for n in range(4, NBATCH):
             front(n)
-            back(n - GN)
-            if n % GN == GN - 1:
-                group_stage(n // GN)
-        for n in range(NBATCH - GN, NBATCH):
-            back(n)
+            for nb in range(done, min(done + 2, ready)):
+                back(nb)
+            done = min(done + 2, ready)
+            n0, gn = GROUPS[group_of[n]]
+            if n == n0 + gn - 1:
+                group_stage(group_of[n])
+                ready = n0 + gn
+        for nb in range(done, NBATCH):
+            back(nb)

@@ -18,6 +18,7 @@ P = 128
 NBATCH = 16
 GROUPS = ((0, 4), (4, 4), (8, 4), (12, 2), (14, 2))
 NB = 19
+CHUNKS = ((0, 4, "s"), (4, 8, "g"), (8, 12, "s"), (12, 16, "g"), (16, 19, "v"))
 FLOPS = 2 * 1024 * 256 * (8192 + 9 * 1024 + 9 * 128)
 
 
@@ -29,12 +30,13 @@ def tile_seteq3to3_t_kernel(tc, x, coefs, bias, out):
     b_v = bias.rearrange("o (m p) a b c -> (o m) (p a b c)", m=2, p=P)
 
     with ExitStack() as ctx:
+        ctx.enter_context(tc.manual_schedule())
         keep = ctx.enter_context(tc.tile_pool(name="keep", bufs=1))
         xin = ctx.enter_context(tc.tile_pool(name="xin", bufs=3))
         xtp = ctx.enter_context(tc.tile_pool(name="xtp", bufs=2))
         xgp = ctx.enter_context(tc.tile_pool(name="xgp", bufs=2))
         xcd = ctx.enter_context(tc.tile_pool(name="xcd", bufs=6))
-        s1p = ctx.enter_context(tc.tile_pool(name="s1p", bufs=2))
+        s1p = ctx.enter_context(tc.tile_pool(name="s1p", bufs=1))
         agp = ctx.enter_context(tc.tile_pool(name="agp", bufs=2))
         pst = ctx.enter_context(tc.psum_pool(name="pst", bufs=2))
         psa = ctx.enter_context(tc.psum_pool(name="psa", bufs=2))
@@ -44,19 +46,311 @@ def tile_seteq3to3_t_kernel(tc, x, coefs, bias, out):
         cq = keep.tile([P, 4 * NB * P], U32, align_bytes=64, name="cq")
         cs = keep.tile([P, 4 * NB * P], U8, align_bytes=64, name="cs")
 
+        group_of = {}
+        stage_at = {}
+        quant_at = {}
+        for gi, (n0, gn) in enumerate(GROUPS):
+            for n in range(n0, n0 + gn):
+                group_of[n] = gi
+            quant_at[n0 + gn] = gi
+            stage_at[n0 + gn + 1] = gi
+
         raws = {}
+        craws = {}
+        xgs = {}
+        xts = {}
+        sas = {}
+        svs = {}
+        agrs = {}
+        xqs = {}
+        gcodes = {}
+        psbs = {}
+        bbs = {}
+
+        def live(n):
+            return 0 <= n < NBATCH
 
         def load(n):
-            raw = xin.tile([P, 4096], BF16, name="raw")
-            nc.sync.dma_start(out=raw[:].rearrange("p (g w) -> p g w", g=2), in_=x_v[n])
-            raws[n] = raw
+            if live(n):
+                raw = xin.tile([P, 4096], BF16, name="raw")
+                nc.sync.dma_start(out=raw[:].rearrange("p (g w) -> p g w", g=2), in_=x_v[n])
+                raws[n] = raw
+
+        def agr_view(n):
+            grp = group_of[n]
+            n0, gn = GROUPS[grp]
+            if grp not in agrs:
+                agrs[grp] = agp.tile([P, 3, 2048], BF16, align_bytes=64, name="agr")
+            return agrs[grp][:, :, 0 : gn * 512].rearrange("p a (g n q t) -> p a g n q t", g=2, n=gn, t=4), n - n0
+
+        def regroup(n, who):
+            if not live(n) or who != ("v" if n < 4 else "s"):
+                return
+            xgs[n] = []
+            for g in range(2):
+                xg = xgp.tile([P, 2048], BF16, align_bytes=64, name="xg%d" % g)
+                dst = xg[:].rearrange("p (c i t) -> p c t i", i=4, t=4)
+                src = raws[n][:, g * 2048 : (g + 1) * 2048].rearrange("p (t c i) -> p c t i", t=4, i=4)
+                if who == "v":
+                    nc.vector.tensor_copy(out=dst, in_=src)
+                else:
+                    nc.scalar.copy(out=dst, in_=src)
+                xgs[n].append(xg)
+
+        def transposes(n, u):
+            if not live(n):
+                return
+            if u == 0:
+                xts[n] = xtp.tile([P, 4096], BF16, name="xT")
+            tp = pst.tile([P, 1024], BF16, name="tp")
+            for r in range(8):
+                o = (u * 8 + r) * P
+                nc.tensor.transpose(tp[:, r * P : (r + 1) * P], raws[n][:, o : o + P], ident[:])
+            nc.scalar.copy(out=xts[n][:, u * 1024 : (u + 1) * 1024], in_=tp[:])
+
+        def sums(n, g, h):
+            if not live(n):
+                return
+            if g == 0 and h == 0:
+                svs[n] = psv.tile([P, 512], F32, name="sv")
+            if h == 0:
+                sas[(n, g)] = psa.tile([P, 512], F32, name="sa")
+            sa = sas[(n, g)]
+            sv = svs[n]
+            for t in (2 * h, 2 * h + 1):
+                for c in range(4):
+                    o = ((g * 4 + t) * 4 + c) * P
+                    nc.tensor.matmul(
+                        out=sa[:, (t * 4 + c) * 32 : (t * 4 + c + 1) * 32],
+                        lhsT=xts[n][:, o : o + P], rhs=sb[:, 0:32], start=True, stop=True,
+                    )
+                    nc.tensor.matmul(
+                        out=sv[:, (g * 4 + t) * 24 : (g * 4 + t + 1) * 24],
+                        lhsT=xts[n][:, o : o + P], rhs=sb[:, 32 + 24 * c : 56 + 24 * c], start=(c == 0), stop=(c == 3),
+                    )
+
+        def sums_out(n, g):
+            if not live(n):
+                return
+            agr_v, ni = agr_view(n)
+            sa_v = sas[(n, g)][:].rearrange("p (t c a e) -> p a c e t", t=4, c=4, a=2)
+            for a in range(2):
+                nc.scalar.copy(out=agr_v[:, 1 + a, g, ni].rearrange("p (c e) t -> p c e t", c=4), in_=sa_v[:, a])
+            nc.scalar.copy(
+                out=vgr_v[:, :, g, ni * 8 : (ni + 1) * 8, :],
+                in_=svs[n][:, g * 96 : (g + 1) * 96].rearrange("p (t v r) -> p v r t", t=4, v=3),
+            )
+
+        def sum_over_i(n):
+            if not live(n):
+                return
+            agr_v, ni = agr_view(n)
+            s1 = s1p.tile([P, 2, 2, 256], F32, name="s1")
+            for g in range(2):
+                nc.vector.tensor_reduce(
+                    out=s1[:, g], in_=xgs[n][g][:].rearrange("p (h i e) -> p h e i", h=2, i=4), axis=AX, op=ADD
+                )
+            with nc.allow_low_precision(reason="the sum is made in float32 and rounded once to bfloat16"):
+                nc.vector.tensor_reduce(
+                    out=agr_v[:, 0, :, ni].rearrange("p g q t -> p g (q t)"),
+                    in_=s1[:].rearrange("p g h e -> p g e h"), axis=AX, op=ADD,
+                )
+
+        def quantise_x(n):
+            if not live(n):
+                return
+            xq = xcd.tile([P, 1024], U32, align_bytes=64, name="xq")
+            xs = xcd.tile([P, 1024], U8, align_bytes=64, name="xs")
+            for g in range(2):
+                nc.vector.quantize_mx(
+                    out=xq[:, g * 512 : (g + 1) * 512].bitcast(FP8X4), scales=xs[:, g * 512 : (g + 1) * 512], in_=xgs[n][g][:]
+                )
+            xqs[n] = (xq, xs)
+
+        def cload(cst, step):
+            if step < 4:
+                m, g = divmod(step, 2)
+                craw = cst.tile([P, 4, 128 * NB], BF16, name="craw")
+                nc.sync.dma_start(out=craw[:], in_=c_v[g][:, :, m * 128 * NB : (m + 1) * 128 * NB])
+                craws[step] = craw
+
+        def coef_regroup(cst, step):
+            src = craws[step][:].rearrange("p t (s b) -> p b s t", b=NB)
+            tiles = []
+            for b0, b1, who in CHUNKS:
+                cgr = cst.tile([P, 2048], BF16, align_bytes=64, name="cgr_" + who)
+                dst = cgr[:, 0 : (b1 - b0) * 512].rearrange("p (b s t) -> p b s t", b=b1 - b0, t=4)
+                if who == "s":
+                    nc.scalar.copy(out=dst, in_=src[:, b0:b1])
+                elif who == "g":
+                    nc.gpsimd.tensor_scalar(out=dst, in0=src[:, b0:b1], scalar1=1.0, scalar2=0.0, op0=MULT, op1=ADD)
+                else:
+                    nc.vector.tensor_copy(out=dst, in_=src[:, b0:b1])
+                tiles.append(cgr)
+            return tiles
+
+        def coef_quantise(step, tiles):
+            m, g = divmod(step, 2)
+            base = (g * 2 + m) * NB * P
+            for (b0, b1, who), cgr in zip(CHUNKS, tiles):
+                pieces = ((0, 4),) if b1 - b0 == 4 else ((0, 2), (2, 3))
+                for q0, q1 in pieces:
+                    nc.vector.quantize_mx(
+                        out=cq[:, base + (b0 + q0) * P : base + (b0 + q1) * P].bitcast(FP8X4),
+                        scales=cs[:, base + (b0 + q0) * P : base + (b0 + q1) * P],
+                        in_=cgr[:, q0 * 512 : q1 * 512],
+                    )
+
+        def cw(g, m, b):
+            o = ((g * 2 + m) * NB + b) * P
+            return cq[:, o : o + P].bitcast(FP8X4), cs[:, o : o + P]
+
+        def group_quantise(late, grp):
+            gn = GROUPS[grp][1]
+            agr = agrs[grp]
+            aq = late.tile([P, 1536], U32, align_bytes=64, name="aq")
+            asc = late.tile([P, 1536], U8, align_bytes=64, name="asc")
+            vq = late.tile([P, 768], U32, align_bytes=64, name="vq")
+            vs = late.tile([P, 768], U8, align_bytes=64, name="vs")
+            nc.vector.quantize_mx(out=vq[:, 0:512].bitcast(FP8X4), scales=vs[:, 0:512], in_=vgr[:, 0:2048])
+            nc.vector.quantize_mx(out=vq[:, 512:768].bitcast(FP8X4), scales=vs[:, 512:768], in_=vgr[:, 2048:3072])
+            for a3 in range(3):
+                nc.vector.quantize_mx(
+                    out=aq[:, a3 * 512 : a3 * 512 + gn * 128].bitcast(FP8X4),
+                    scales=asc[:, a3 * 512 : a3 * 512 + gn * 128],
+                    in_=agr[:, a3, 0 : gn * 512],
+                )
+            gcodes[grp] = (aq, asc, vq, vs)
+
+        def a_group(acc, grp, m, pl):
+            aq, asc, vq, vs = gcodes[grp]
+            nw = GROUPS[grp][1] * 64
+            for idx in range(6):
+                a3, g = divmod(idx, 2)
+                w, wsc = cw(g, m, 1 + 3 * a3 + pl)
+                o = a3 * 512 + g * nw
+                nc.tensor.matmul_mx(
+                    out=acc, lhsT=w, lhsT_scale=wsc,
+                    rhs=aq[:, o : o + nw].bitcast(FP8X4), rhs_scale=asc[:, o : o + nw],
+                    start=(idx == 0), stop=(idx == 5),
+                )
+
+        def q_products(late, grp):
+            gn = GROUPS[grp][1]
+            aq, asc, vq, vs = gcodes[grp]
+            qsbs = []
+            for m in range(2):
+                qsb = late.tile([P, 3, 32], F32, name="qsb%d" % m)
+                qps = psx.tile([P, 512], F32, name="qps", tag="mx")
+                for pl in range(3):
+                    for idx in range(6):
+                        a3, g = divmod(idx, 2)
+                        w, wsc = cw(g, m, 10 + 3 * a3 + pl)
+                        o = (a3 * 2 + g) * P
+                        nc.tensor.matmul_mx(
+                            out=qps[:, pl * P : (pl + 1) * P], lhsT=w, lhsT_scale=wsc,
+                            rhs=vq[:, o : o + P].bitcast(FP8X4), rhs_scale=vs[:, o : o + P],
+                            start=(idx == 0), stop=(idx == 5),
+                        )
+                nc.scalar.copy(
+                    out=qsb[:, :, 0 : gn * 8], in_=qps[:, 0:384].rearrange("p (l c) -> p l c", l=3)[:, :, 0 : gn * 8]
+                )
+                qsbs.append(qsb)
+            return qsbs
+
+        def p_products(late, grp, m, qsb):
+            nw = GROUPS[grp][1] * 64
+            if m >= 0:
+                p10 = late.tile([P, 2, 256], F32, name="p10_%d" % m)
+                p2 = late.tile([P, 256], F32, name="p2_%d" % m)
+                pps = psx.tile([P, 512], F32, name="pps", tag="mx")
+                a_group(pps[:, 0:nw], grp, m, 1)
+                a_group(pps[:, 256 : 256 + nw], grp, m, 0)
+                pp2 = psx.tile([P, 512], F32, name="pp2", tag="mx")
+                a_group(pp2[:, 0:nw], grp, m, 2)
+                nc.scalar.activation(out=p2[:, 0:nw], in_=pp2[:, 0:nw], func=IDENT, bias=bias_sb[:, m : m + 1])
+                psbs[(grp, m)] = (p10, p2)
+            return (pps, qsb, p10)
+
+        def fold(grp, item):
+            gn = GROUPS[grp][1]
+            nw = gn * 64
+            pps, qsb, p10 = item
+            nc.vector.tensor_tensor(
+                out=p10[:, :, 0:nw].rearrange("p l (e k) -> p l e k", k=8),
+                in0=pps[:].rearrange("p (l c) -> p l c", l=2)[:, :, 0:nw].rearrange("p l (e k) -> p l e k", k=8),
+                in1=qsb[:, 0:2, 0 : gn * 8].unsqueeze(3).to_broadcast([P, 2, gn * 8, 8]),
+                op=ADD,
+            )
+            nc.gpsimd.tensor_tensor(
+                out=p10[:, 1, 0:nw].rearrange("p (n j k) -> p n j k", n=gn, k=8),
+                in0=p10[:, 1, 0:nw].rearrange("p (n j k) -> p n j k", n=gn, k=8),
+                in1=qsb[:, 2, 0 : gn * 8].rearrange("p (n k) -> p n k", n=gn).unsqueeze(2).to_broadcast([P, gn, 8, 8]),
+                op=ADD,
+            )
+
+        def spread(n, m):
+            grp = group_of[n]
+            ni = n - GROUPS[grp][0]
+            p10, p2 = psbs[(grp, m)]
+            sl = slice(ni * 64, (ni + 1) * 64)
+            p0b = p10[:, 1, sl].rearrange("p (j k) -> p j k", j=8).unsqueeze(1).to_broadcast([P, 8, 8, 8])
+            p1b = p10[:, 0, sl].rearrange("p (i k) -> p i k", i=8).unsqueeze(2).to_broadcast([P, 8, 8, 8])
+            p2b = p2[:, sl].unsqueeze(2).to_broadcast([P, 64, 8])
+            return p0b, p1b, p2b
+
+        def back_gpsimd(bp1, bp2, n):
+            last = group_of[n] == len(GROUPS) - 1
+            bbs[n] = []
+            for m in range(2):
+                p0b, p1b, p2b = spread(n, m)
+                on_vector = last and m == 1
+                b2 = None
+                if not on_vector:
+                    b1 = bp1.tile([P, 512], F32, name="b1")
+                    b2 = bp2.tile([P, 512], F32, name="b2")
+                    nc.gpsimd.tensor_tensor(out=b1[:].rearrange("p (i j k) -> p i j k", i=8, j=8), in0=p0b, in1=p1b, op=ADD)
+                    nc.gpsimd.tensor_tensor(
+                        out=b2[:].rearrange("p (e k) -> p e k", k=8), in0=b1[:].rearrange("p (e k) -> p e k", k=8), in1=p2b, op=ADD
+                    )
+                bbs[n].append(b2)
+
+        def back_finish(late, bp1, bp2, n):
+            xq, xs = xqs[n]
+            osb = late.tile([P, 2, 512], F32, name="osb")
+            for m in range(2):
+                p0b, p1b, p2b = spread(n, m)
+                b2 = bbs[n][m]
+                mps = psx.tile([P, 512], F32, name="mps", tag="mx")
+                for g in range(2):
+                    w, wsc = cw(g, m, 0)
+                    nc.tensor.matmul_mx(
+                        out=mps[:], lhsT=w, lhsT_scale=wsc,
+                        rhs=xq[:, g * 512 : (g + 1) * 512].bitcast(FP8X4), rhs_scale=xs[:, g * 512 : (g + 1) * 512],
+                        start=(g == 0), stop=(g == 1),
+                    )
+                if b2 is None:
+                    b1 = bp1.tile([P, 512], F32, name="b1")
+                    b2 = bp2.tile([P, 512], F32, name="b2")
+                    nc.vector.tensor_tensor(
+                        out=b1[:].rearrange("p (i j k) -> p i j k", i=8, j=8),
+                        in0=mps[:].rearrange("p (i j k) -> p i j k", i=8, j=8), in1=p0b, op=ADD,
+                    )
+                    nc.vector.tensor_tensor(
+                        out=b2[:].rearrange("p (i j k) -> p i j k", i=8, j=8),
+                        in0=b1[:].rearrange("p (i j k) -> p i j k", i=8, j=8), in1=p1b, op=ADD,
+                    )
+                    nc.vector.tensor_tensor(
+                        out=osb[:, m].rearrange("p (e k) -> p e k", k=8), in0=b2[:].rearrange("p (e k) -> p e k", k=8), in1=p2b, op=ADD
+                    )
+                else:
+                    nc.vector.tensor_tensor(out=osb[:, m], in0=mps[:], in1=b2[:], op=ADD)
+            nc.sync.dma_start(out=o_v[n], in_=osb[:])
 
         load(0)
         load(1)
-
         ident = keep.tile([P, P], BF16, name="ident")
         make_identity(nc, ident[:])
-
         sf = keep.tile([P, P], F32, name="sf")
         nc.vector.memset(sf[:], 0.0)
         nc.vector.tensor_reduce(
@@ -75,245 +369,89 @@ def tile_seteq3to3_t_kernel(tc, x, coefs, bias, out):
             )
         sb = keep.tile([P, P], BF16, name="sb")
         nc.vector.tensor_copy(out=sb[:], in_=sf[:])
-
+        vgr = keep.tile([P, 3072], BF16, align_bytes=64, name="vgr")
+        nc.vector.memset(vgr[:], 0.0)
+        vgr_v = vgr[:].rearrange("p (v g c t) -> p v g c t", v=3, g=2, t=4)
         bz = keep.tile([P, P], BF16, name="bz")
         nc.vector.memset(bz[:], 0.0)
-        nc.sync.dma_start(out=bz[0:2, :], in_=b_v)
-        bps = pst.tile([P, 1024], BF16, name="bps", tag="tp")
-        nc.tensor.transpose(bps[:, 0:P], bz[:], ident[:])
         bias_sb = keep.tile([P, 2], F32, name="bias_sb")
-        nc.vector.tensor_copy(out=bias_sb[:], in_=bps[:, 0:2])
 
-        vgrs = []
-        for h in range(2):
-            vgr = keep.tile([P, 3072], BF16, align_bytes=64, name="vgr%d" % h)
-            nc.vector.memset(vgr[:], 0.0)
-            vgrs.append(vgr)
+        def bias_setup():
+            nc.sync.dma_start(out=bz[0:2, :], in_=b_v)
+            bps = pst.tile([P, 1024], BF16, name="bps", tag="tp")
+            nc.tensor.transpose(bps[:, 0:P], bz[:], ident[:])
+            nc.vector.tensor_copy(out=bias_sb[:], in_=bps[:, 0:2])
 
-        agrs = {}
-        group_of = {}
-        for gi, (n0, gn) in enumerate(GROUPS):
-            for n in range(n0, n0 + gn):
-                group_of[n] = gi
-        xqs = {}
+        state = {"fold": None, "cgr": [], "to_g": [], "to_f": []}
 
-        def front(n):
-            grp = group_of[n]
-            n0, gn = GROUPS[grp]
-            ni = n - n0
-            if n + 2 < NBATCH:
-                load(n + 2)
-            raw = raws[n]
-            if ni == 0:
-                agrs[grp] = agp.tile([P, 3, 2048], BF16, align_bytes=64, name="agr")
-            agr_v = agrs[grp][:, :, 0 : gn * 512].rearrange("p a (g n q t) -> p a g n q t", g=2, n=gn, t=4)
-            xgs = []
-            for g in range(2):
-                xg = xgp.tile([P, 2048], BF16, align_bytes=64, name="xg%d" % g)
-                dst = xg[:].rearrange("p (c i t) -> p c t i", i=4, t=4)
-                src = raw[:, g * 2048 : (g + 1) * 2048].rearrange("p (t c i) -> p c t i", t=4, i=4)
-                if g == 0:
-                    nc.vector.tensor_copy(out=dst, in_=src)
-                else:
-                    nc.scalar.copy(out=dst, in_=src)
-                xgs.append(xg)
-            vgr_v = vgrs[grp % 2][:].rearrange("p (v g c t) -> p v g c t", v=3, g=2, t=4)
-            xT = xtp.tile([P, 4096], BF16, name="xT")
-            for u in range(4):
-                tp = pst.tile([P, 1024], BF16, name="tp")
-                for r in range(8):
-                    o = (u * 8 + r) * P
-                    nc.tensor.transpose(tp[:, r * P : (r + 1) * P], raw[:, o : o + P], ident[:])
-                nc.scalar.copy(out=xT[:, u * 1024 : (u + 1) * 1024], in_=tp[:])
-            s1 = s1p.tile([P, 2, 2, 256], F32, name="s1")
-            for g in range(2):
-                nc.vector.tensor_reduce(
-                    out=s1[:, g], in_=xgs[g][:].rearrange("p (h i e) -> p h e i", h=2, i=4), axis=AX, op=ADD
-                )
-            nc.vector.tensor_tensor(
-                out=agr_v[:, 0, :, ni].rearrange("p g q t -> p g (q t)"), in0=s1[:, :, 0], in1=s1[:, :, 1], op=ADD
-            )
-            sv = psv.tile([P, 512], F32, name="sv")
-            for g in range(2):
-                sa = psa.tile([P, 512], F32, name="sa")
-                for t in range(4):
-                    for c in range(4):
-                        o = ((g * 4 + t) * 4 + c) * P
-                        nc.tensor.matmul(
-                            out=sa[:, (t * 4 + c) * 32 : (t * 4 + c + 1) * 32],
-                            lhsT=xT[:, o : o + P], rhs=sb[:, 0:32], start=True, stop=True,
-                        )
-                        nc.tensor.matmul(
-                            out=sv[:, (g * 4 + t) * 24 : (g * 4 + t + 1) * 24],
-                            lhsT=xT[:, o : o + P], rhs=sb[:, 32 + 24 * c : 56 + 24 * c], start=(c == 0), stop=(c == 3),
-                        )
-                sa_v = sa[:].rearrange("p (t c a e) -> p a c e t", t=4, c=4, a=2)
-                for a in range(2):
-                    nc.scalar.copy(
-                        out=agr_v[:, 1 + a, g, ni].rearrange("p (c e) t -> p c e t", c=4), in_=sa_v[:, a]
-                    )
-                nc.scalar.copy(
-                    out=vgr_v[:, :, g, ni * 8 : (ni + 1) * 8, :],
-                    in_=sv[:, g * 96 : (g + 1) * 96].rearrange("p (t v r) -> p v r t", t=4, v=3),
-                )
-            xq = xcd.tile([P, 1024], U32, align_bytes=64, name="xq")
-            xs = xcd.tile([P, 1024], U8, align_bytes=64, name="xs")
-            for g in range(2):
-                nc.vector.quantize_mx(
-                    out=xq[:, g * 512 : (g + 1) * 512].bitcast(FP8X4), scales=xs[:, g * 512 : (g + 1) * 512], in_=xgs[g][:]
-                )
-            xqs[n] = (xq, xs)
+        def step_a(k, cst, late):
+            n = k
+            m = k - 1
+            load(k + 2)
+            grp = stage_at.get(k)
+            if grp is not None:
+                for g in range(2):
+                    for h in range(2):
+                        sums(m, g, h)
+                sums_out(m, 0)
+                sums_out(m, 1)
+                regroup(n, "s")
+                sum_over_i(m)
+                qsbs = q_products(late, grp)
+                fold(grp, p_products(late, grp, 0, qsbs[0]))
+                state["fold"] = p_products(late, grp, 1, qsbs[1])
+            transposes(n, 0)
+            transposes(n, 1)
+            if grp is None:
+                sums(m, 0, 0)
+            transposes(n, 2)
+            if grp is None:
+                sums(m, 0, 1)
+            transposes(n, 3)
+            if grp is None:
+                sums(m, 1, 0)
+                sums(m, 1, 1)
+                sums_out(m, 0)
+                sums_out(m, 1)
+                regroup(n, "s")
+                sum_over_i(m)
+            regroup(n, "v")
+            quantise_x(m)
+            if state["cgr"]:
+                step, tiles = state["cgr"][0]
+                state["cgr"] = []
+                coef_quantise(step, tiles)
+            if k < 4:
+                state["cgr"] = [(k, coef_regroup(cst, k))]
+                cload(cst, k + 2)
+
+        def step_b(k, late, bp1, bp2):
+            grp = stage_at.get(k)
+            if grp is not None:
+                fold(grp, state["fold"])
+                n0, gn = GROUPS[grp]
+                state["to_g"] = state["to_g"] + list(range(n0, n0 + gn))
+            if k in quant_at:
+                group_quantise(late, quant_at[k])
+            for n in state["to_f"][0:2]:
+                back_finish(late, bp1, bp2, n)
+            state["to_f"] = state["to_f"][2:]
+            for n in state["to_g"][0:2]:
+                back_gpsimd(bp1, bp2, n)
+                state["to_f"] = state["to_f"] + [n]
+            state["to_g"] = state["to_g"][2:]
 
         with tc.tile_pool(name="cst", bufs=2) as cst:
-            for step in range(4):
-                m, g = divmod(step, 2)
-                craw = cst.tile([P, 4, 128 * NB], BF16, name="craw")
-                nc.gpsimd.dma_start(out=craw[:], in_=c_v[g][:, :, m * 128 * NB : (m + 1) * 128 * NB])
-                front(step)
-                src = craw[:].rearrange("p t (s b) -> p b s t", b=NB)
-                base = (g * 2 + m) * NB * P
-                for b0, b1, who in ((0, 8, "s"), (8, 16, "g"), (16, 19, "v")):
-                    cgr = cst.tile([P, 4096], BF16, align_bytes=64, name="cgr")
-                    dst = cgr[:, 0 : (b1 - b0) * 512].rearrange("p (b s t) -> p b s t", b=b1 - b0, t=4)
-                    if who == "s":
-                        nc.scalar.copy(out=dst, in_=src[:, b0:b1])
-                    elif who == "g":
-                        nc.gpsimd.tensor_scalar(out=dst, in0=src[:, b0:b1], scalar1=1.0, scalar2=0.0, op0=MULT, op1=ADD)
-                    else:
-                        nc.vector.tensor_copy(out=dst, in_=src[:, b0:b1])
-                    pieces = ((0, 8),) if b1 - b0 == 8 else ((0, 2), (2, 3))
-                    for q0, q1 in pieces:
-                        nc.vector.quantize_mx(
-                            out=cq[:, base + (b0 + q0) * P : base + (b0 + q1) * P].bitcast(FP8X4),
-                            scales=cs[:, base + (b0 + q0) * P : base + (b0 + q1) * P],
-                            in_=cgr[:, q0 * 512 : q1 * 512],
-                        )
-
-        def cw(g, m, b):
-            o = ((g * 2 + m) * NB + b) * P
-            return cq[:, o : o + P].bitcast(FP8X4), cs[:, o : o + P]
-
+            cload(cst, 0)
+            cload(cst, 1)
+            for k in range(5):
+                step_a(k, cst, None)
+                if k == 2:
+                    bias_setup()
         late = ctx.enter_context(tc.tile_pool(name="late", bufs=2))
-        psbs = {}
-
-        def group_stage(grp):
-            gn = GROUPS[grp][1]
-            agr = agrs[grp]
-            vgr = vgrs[grp % 2]
-            aq = late.tile([P, 1536], U32, align_bytes=64, name="aq")
-            asc = late.tile([P, 1536], U8, align_bytes=64, name="asc")
-            vq = late.tile([P, 768], U32, align_bytes=64, name="vq")
-            vs = late.tile([P, 768], U8, align_bytes=64, name="vs")
-            nc.vector.quantize_mx(out=vq[:, 0:512].bitcast(FP8X4), scales=vs[:, 0:512], in_=vgr[:, 0:2048])
-            nc.vector.quantize_mx(out=vq[:, 512:768].bitcast(FP8X4), scales=vs[:, 512:768], in_=vgr[:, 2048:3072])
-            for a3 in range(3):
-                nc.vector.quantize_mx(
-                    out=aq[:, a3 * 512 : a3 * 512 + gn * 128].bitcast(FP8X4),
-                    scales=asc[:, a3 * 512 : a3 * 512 + gn * 128],
-                    in_=agr[:, a3, 0 : gn * 512],
-                )
-            for m in range(2):
-                qsb = late.tile([P, 3, 32], F32, name="qsb%d" % m)
-                for pl in range(3):
-                    qps = psx.tile([P, 512], F32, name="qps", tag="mx")
-                    for idx in range(6):
-                        a3, g = divmod(idx, 2)
-                        w, wsc = cw(g, m, 10 + 3 * a3 + pl)
-                        o = (a3 * 2 + g) * P
-                        nc.tensor.matmul_mx(
-                            out=qps[:, 0:P], lhsT=w, lhsT_scale=wsc,
-                            rhs=vq[:, o : o + P].bitcast(FP8X4), rhs_scale=vs[:, o : o + P],
-                            start=(idx == 0), stop=(idx == 5),
-                        )
-                    if pl == 0:
-                        nc.scalar.activation(out=qsb[:, 0, 0 : gn * 8], in_=qps[:, 0 : gn * 8], func=IDENT, bias=bias_sb[:, m : m + 1])
-                    else:
-                        nc.scalar.copy(out=qsb[:, pl, 0 : gn * 8], in_=qps[:, 0 : gn * 8])
-                psb = late.tile([P, 3, 256], F32, name="psb%d" % m)
-                nw = gn * 64
-                for pl in range(3):
-                    pps = psx.tile([P, 512], F32, name="pps", tag="mx")
-                    for idx in range(6):
-                        a3, g = divmod(idx, 2)
-                        w, wsc = cw(g, m, 1 + 3 * a3 + pl)
-                        o = a3 * 512 + g * nw
-                        nc.tensor.matmul_mx(
-                            out=pps[:, 0:nw], lhsT=w, lhsT_scale=wsc,
-                            rhs=aq[:, o : o + nw].bitcast(FP8X4), rhs_scale=asc[:, o : o + nw],
-                            start=(idx == 0), stop=(idx == 5),
-                        )
-                    if pl == 2:
-                        nc.scalar.copy(out=psb[:, 2, 0:nw], in_=pps[:, 0:nw])
-                    else:
-                        nc.vector.tensor_tensor(
-                            out=psb[:, pl, 0:nw].rearrange("p (e k) -> p e k", k=8),
-                            in0=pps[:, 0:nw].rearrange("p (e k) -> p e k", k=8),
-                            in1=qsb[:, 1 - pl, 0 : gn * 8].unsqueeze(2).to_broadcast([P, gn * 8, 8]),
-                            op=ADD,
-                        )
-                nc.vector.tensor_tensor(
-                    out=psb[:, 0, 0:nw].rearrange("p (n j k) -> p n j k", n=gn, k=8),
-                    in0=psb[:, 0, 0:nw].rearrange("p (n j k) -> p n j k", n=gn, k=8),
-                    in1=qsb[:, 2, 0 : gn * 8].rearrange("p (n k) -> p n k", n=gn).unsqueeze(2).to_broadcast([P, gn, 8, 8]),
-                    op=ADD,
-                )
-                psbs[(grp, m)] = psb
-
-        def back(n):
-            grp = group_of[n]
-            ni = n - GROUPS[grp][0]
-            last = grp == len(GROUPS) - 1
-            xq, xs = xqs[n]
-            osb = late.tile([P, 2, 512], F32, name="osb")
-            sl = slice(ni * 64, (ni + 1) * 64)
-            for m in range(2):
-                psb = psbs[(grp, m)]
-                p0b = psb[:, 0, sl].rearrange("p (j k) -> p j k", j=8).unsqueeze(1).to_broadcast([P, 8, 8, 8])
-                p1b = psb[:, 1, sl].rearrange("p (i k) -> p i k", i=8).unsqueeze(2).to_broadcast([P, 8, 8, 8])
-                p2b = psb[:, 2, sl].unsqueeze(2).to_broadcast([P, 64, 8])
-                b1 = late.tile([P, 512], F32, name="b1")
-                b2 = late.tile([P, 512], F32, name="b2")
-                on_vector = last and m == 1
-                if not on_vector:
-                    nc.gpsimd.tensor_tensor(out=b1[:].rearrange("p (i j k) -> p i j k", i=8, j=8), in0=p0b, in1=p1b, op=ADD)
-                    nc.gpsimd.tensor_tensor(
-                        out=b2[:].rearrange("p (e k) -> p e k", k=8), in0=b1[:].rearrange("p (e k) -> p e k", k=8), in1=p2b, op=ADD
-                    )
-                mps = psx.tile([P, 512], F32, name="mps", tag="mx")
-                for g in range(2):
-                    w, wsc = cw(g, m, 0)
-                    nc.tensor.matmul_mx(
-                        out=mps[:], lhsT=w, lhsT_scale=wsc,
-                        rhs=xq[:, g * 512 : (g + 1) * 512].bitcast(FP8X4), rhs_scale=xs[:, g * 512 : (g + 1) * 512],
-                        start=(g == 0), stop=(g == 1),
-                    )
-                if on_vector:
-                    nc.vector.tensor_tensor(
-                        out=b1[:].rearrange("p (i j k) -> p i j k", i=8, j=8),
-                        in0=mps[:].rearrange("p (i j k) -> p i j k", i=8, j=8), in1=p0b, op=ADD,
-                    )
-                    nc.vector.tensor_tensor(
-                        out=b2[:].rearrange("p (i j k) -> p i j k", i=8, j=8),
-                        in0=b1[:].rearrange("p (i j k) -> p i j k", i=8, j=8), in1=p1b, op=ADD,
-                    )
-                    nc.vector.tensor_tensor(
-                        out=osb[:, m].rearrange("p (e k) -> p e k", k=8), in0=b2[:].rearrange("p (e k) -> p e k", k=8), in1=p2b, op=ADD
-                    )
-                else:
-                    nc.vector.tensor_tensor(out=osb[:, m], in0=mps[:], in1=b2[:], op=ADD)
-            nc.sync.dma_start(out=o_v[n], in_=osb[:])
-
-        group_stage(0)
-        ready = 4
-        done = 0
-        for n in range(4, NBATCH):
-            front(n)
-            for nb in range(done, min(done + 2, ready)):
-                back(nb)
-            done = min(done + 2, ready)
-            n0, gn = GROUPS[group_of[n]]
-            if n == n0 + gn - 1:
-                group_stage(group_of[n])
-                ready = n0 + gn
-        for nb in range(done, NBATCH):
-            back(nb)
+        bp1 = ctx.enter_context(tc.tile_pool(name="bp1", bufs=2))
+        bp2 = ctx.enter_context(tc.tile_pool(name="bp2", bufs=4))
+        step_b(4, late, bp1, bp2)
+        for k in range(5, NBATCH + 6):
+            step_a(k, None, late)
+            step_b(k, late, bp1, bp2)

@@ -175,17 +175,17 @@ def tile_seteq3to3_t_kernel(tc, x, coefs, bias, out):
                 craws[step] = craw
 
         def coef_regroup(cst, step):
-            src = craws[step][:].rearrange("p t (s b) -> p b s t", b=NB)
+            src = craws[step][:].rearrange("p t (s b) -> p s t b", b=NB)
             tiles = []
             for b0, b1, who in CHUNKS:
                 cgr = cst.tile([P, 2048], BF16, align_bytes=64, name="cgr_" + who)
-                dst = cgr[:, 0 : (b1 - b0) * 512].rearrange("p (b s t) -> p b s t", b=b1 - b0, t=4)
+                dst = cgr[:, 0 : (b1 - b0) * 512].rearrange("p (b s t) -> p s t b", b=b1 - b0, t=4)
                 if who == "s":
-                    nc.scalar.copy(out=dst, in_=src[:, b0:b1])
+                    nc.scalar.copy(out=dst, in_=src[:, :, :, b0:b1])
                 elif who == "g":
-                    nc.gpsimd.tensor_scalar(out=dst, in0=src[:, b0:b1], scalar1=1.0, scalar2=0.0, op0=MULT, op1=ADD)
+                    nc.gpsimd.tensor_scalar(out=dst, in0=src[:, :, :, b0:b1], scalar1=1.0, scalar2=0.0, op0=MULT, op1=ADD)
                 else:
-                    nc.vector.tensor_copy(out=dst, in_=src[:, b0:b1])
+                    nc.vector.tensor_copy(out=dst, in_=src[:, :, :, b0:b1])
                 tiles.append(cgr)
             return tiles
 

@@ -39,21 +39,23 @@ def tile_seteq3to3_t_kernel(tc, x, coefs, bias, out):
         s1p = ctx.enter_context(tc.tile_pool(name="s1p", bufs=1))
         agp = ctx.enter_context(tc.tile_pool(name="agp", bufs=2))
         pst = ctx.enter_context(tc.psum_pool(name="pst", bufs=2))
-        psa = ctx.enter_context(tc.psum_pool(name="psa", bufs=2))
+        psa = ctx.enter_context(tc.psum_pool(name="psa", bufs=1))
         psv = ctx.enter_context(tc.psum_pool(name="psv", bufs=1))
-        psx = ctx.enter_context(tc.psum_pool(name="psx", bufs=3))
+        psx = ctx.enter_context(tc.psum_pool(name="psx", bufs=4))
 
         cq = keep.tile([P, 4 * NB * P], U32, align_bytes=64, name="cq")
         cs = keep.tile([P, 4 * NB * P], U8, align_bytes=64, name="cs")
 
         group_of = {}
         stage_at = {}
+        fold_at = {}
         quant_at = {}
         for gi, (n0, gn) in enumerate(GROUPS):
             for n in range(n0, n0 + gn):
                 group_of[n] = gi
             quant_at[n0 + gn] = gi
             stage_at[n0 + gn + 1] = gi
+            fold_at[n0 + gn + 2] = gi
 
         raws = {}
         craws = {}
@@ -66,6 +68,7 @@ def tile_seteq3to3_t_kernel(tc, x, coefs, bias, out):
         gcodes = {}
         psbs = {}
         bbs = {}
+        mains = {}
 
         def live(n):
             return 0 <= n < NBATCH
@@ -83,11 +86,12 @@ def tile_seteq3to3_t_kernel(tc, x, coefs, bias, out):
                 agrs[grp] = agp.tile([P, 3, 2048], BF16, align_bytes=64, name="agr")
             return agrs[grp][:, :, 0 : gn * 512].rearrange("p a (g n q t) -> p a g n q t", g=2, n=gn, t=4), n - n0
 
-        def regroup(n, who):
+        def regroup(n, who, halves):
             if not live(n) or who != ("v" if n < 4 else "s"):
                 return
-            xgs[n] = []
-            for g in range(2):
+            if n not in xgs:
+                xgs[n] = []
+            for g in halves:
                 xg = xgp.tile([P, 2048], BF16, align_bytes=64, name="xg%d" % g)
                 dst = xg[:].rearrange("p (c i t) -> p c t i", i=4, t=4)
                 src = raws[n][:, g * 2048 : (g + 1) * 2048].rearrange("p (t c i) -> p c t i", t=4, i=4)
@@ -136,10 +140,12 @@ def tile_seteq3to3_t_kernel(tc, x, coefs, bias, out):
             sa_v = sas[(n, g)][:].rearrange("p (t c a e) -> p a c e t", t=4, c=4, a=2)
             for a in range(2):
                 nc.scalar.copy(out=agr_v[:, 1 + a, g, ni].rearrange("p (c e) t -> p c e t", c=4), in_=sa_v[:, a])
-            nc.scalar.copy(
-                out=vgr_v[:, :, g, ni * 8 : (ni + 1) * 8, :],
-                in_=svs[n][:, g * 96 : (g + 1) * 96].rearrange("p (t v r) -> p v r t", t=4, v=3),
-            )
+            if g == 1:
+                for gg in range(2):
+                    nc.scalar.copy(
+                        out=vgr_v[:, :, gg, ni * 8 : (ni + 1) * 8, :],
+                        in_=svs[n][:, gg * 96 : (gg + 1) * 96].rearrange("p (t v r) -> p v r t", t=4, v=3),
+                    )
 
         def sum_over_i(n):
             if not live(n):
@@ -315,20 +321,24 @@ def tile_seteq3to3_t_kernel(tc, x, coefs, bias, out):
                     )
                 bbs[n].append(b2)
 
-        def back_finish(late, bp1, bp2, n):
+        def main_product(n, m):
             xq, xs = xqs[n]
+            mps = psx.tile([P, 512], F32, name="mps", tag="mx")
+            for g in range(2):
+                w, wsc = cw(g, m, 0)
+                nc.tensor.matmul_mx(
+                    out=mps[:], lhsT=w, lhsT_scale=wsc,
+                    rhs=xq[:, g * 512 : (g + 1) * 512].bitcast(FP8X4), rhs_scale=xs[:, g * 512 : (g + 1) * 512],
+                    start=(g == 0), stop=(g == 1),
+                )
+            mains[(n, m)] = mps
+
+        def back_finish(late, bp1, bp2, n):
             osb = late.tile([P, 2, 512], F32, name="osb")
             for m in range(2):
                 p0b, p1b, p2b = spread(n, m)
                 b2 = bbs[n][m]
-                mps = psx.tile([P, 512], F32, name="mps", tag="mx")
-                for g in range(2):
-                    w, wsc = cw(g, m, 0)
-                    nc.tensor.matmul_mx(
-                        out=mps[:], lhsT=w, lhsT_scale=wsc,
-                        rhs=xq[:, g * 512 : (g + 1) * 512].bitcast(FP8X4), rhs_scale=xs[:, g * 512 : (g + 1) * 512],
-                        start=(g == 0), stop=(g == 1),
-                    )
+                mps = mains[(n, m)]
                 if b2 is None:
                     b1 = bp1.tile([P, 512], F32, name="b1")
                     b2 = bp2.tile([P, 512], F32, name="b2")
@@ -382,40 +392,41 @@ def tile_seteq3to3_t_kernel(tc, x, coefs, bias, out):
             nc.tensor.transpose(bps[:, 0:P], bz[:], ident[:])
             nc.vector.tensor_copy(out=bias_sb[:], in_=bps[:, 0:2])
 
-        state = {"fold": None, "cgr": [], "to_g": [], "to_f": []}
+        state = {"folds": {}, "cgr": [], "to_g": [], "to_f": [], "now": []}
 
         def step_a(k, cst, late):
             n = k
             m = k - 1
             load(k + 2)
-            grp = stage_at.get(k)
+            grp = fold_at.get(k)
             if grp is not None:
-                for g in range(2):
-                    for h in range(2):
-                        sums(m, g, h)
-                sums_out(m, 0)
-                sums_out(m, 1)
-                regroup(n, "s")
-                sum_over_i(m)
-                qsbs = q_products(late, grp)
-                fold(grp, p_products(late, grp, 0, qsbs[0]))
-                state["fold"] = p_products(late, grp, 1, qsbs[1])
+                for item in state["folds"][grp]:
+                    fold(grp, item)
+                n0, gn = GROUPS[grp]
+                state["to_g"] = state["to_g"] + list(range(n0, n0 + gn))
+            state["now"] = state["to_f"][0:2]
+            state["to_f"] = state["to_f"][2:]
+            todo = [(nb, mb) for nb in state["now"] for mb in range(2)]
+            if todo:
+                main_product(todo[0][0], todo[0][1])
             transposes(n, 0)
             transposes(n, 1)
-            if grp is None:
-                sums(m, 0, 0)
+            regroup(n, "s", (0,))
+            sums(m, 0, 0)
+            sums(m, 0, 1)
+            sums_out(m, 0)
+            if len(todo) > 1:
+                main_product(todo[1][0], todo[1][1])
             transposes(n, 2)
-            if grp is None:
-                sums(m, 0, 1)
             transposes(n, 3)
-            if grp is None:
-                sums(m, 1, 0)
-                sums(m, 1, 1)
-                sums_out(m, 0)
-                sums_out(m, 1)
-                regroup(n, "s")
-                sum_over_i(m)
-            regroup(n, "v")
+            regroup(n, "s", (1,))
+            sums(m, 1, 0)
+            sums(m, 1, 1)
+            sums_out(m, 1)
+            for nb, mb in todo[2:]:
+                main_product(nb, mb)
+            sum_over_i(m)
+            regroup(n, "v", (0, 1))
             quantise_x(m)
             if state["cgr"]:
                 step, tiles = state["cgr"][0]
@@ -426,16 +437,14 @@ def tile_seteq3to3_t_kernel(tc, x, coefs, bias, out):
                 cload(cst, k + 2)
 
         def step_b(k, late, bp1, bp2):
-            grp = stage_at.get(k)
-            if grp is not None:
-                fold(grp, state["fold"])
-                n0, gn = GROUPS[grp]
-                state["to_g"] = state["to_g"] + list(range(n0, n0 + gn))
+            for n in state["now"]:
+                back_finish(late, bp1, bp2, n)
             if k in quant_at:
                 group_quantise(late, quant_at[k])
-            for n in state["to_f"][0:2]:
-                back_finish(late, bp1, bp2, n)
-            state["to_f"] = state["to_f"][2:]
+            grp = stage_at.get(k)
+            if grp is not None:
+                qsbs = q_products(late, grp)
+                state["folds"][grp] = [p_products(late, grp, mb, qsbs[mb]) for mb in range(2)]
             for n in state["to_g"][0:2]:
                 back_gpsimd(bp1, bp2, n)
                 state["to_f"] = state["to_f"] + [n]

@@ -19,6 +19,7 @@ NBATCH = 16
 GROUPS = ((0, 4), (4, 4), (8, 4), (12, 2), (14, 2))
 NB = 19
 CHUNKS = ((0, 4, "s"), (4, 8, "g"), (8, 12, "s"), (12, 16, "g"), (16, 19, "v"))
+BP2 = 4
 FLOPS = 2 * 1024 * 256 * (8192 + 9 * 1024 + 9 * 128)
 
 
@@ -53,10 +54,12 @@ def tile_seteq3to3_t_kernel(tc, x, coefs, bias, out):
         for gi, (n0, gn) in enumerate(GROUPS):
             for n in range(n0, n0 + gn):
                 group_of[n] = gi
-            quant_at[n0 + gn] = gi
-            stage_at[n0 + gn + 1] = gi
-            fold_at[n0 + gn + 2] = gi
+            done = n0 + gn - (1 if gi == len(GROUPS) - 1 else 0)
+            quant_at[done] = gi
+            stage_at[done + 1] = gi
+            fold_at[done + 2] = gi
 
+        made = set()
         raws = {}
         craws = {}
         xgs = {}
@@ -113,8 +116,9 @@ def tile_seteq3to3_t_kernel(tc, x, coefs, bias, out):
             nc.scalar.copy(out=xts[n][:, u * 1024 : (u + 1) * 1024], in_=tp[:])
 
         def sums(n, g, h):
-            if not live(n):
+            if not live(n) or (n, g, h) in made:
                 return
+            made.add((n, g, h))
             if g == 0 and h == 0:
                 svs[n] = psv.tile([P, 512], F32, name="sv")
             if h == 0:
@@ -134,8 +138,9 @@ def tile_seteq3to3_t_kernel(tc, x, coefs, bias, out):
                     )
 
         def sums_out(n, g):
-            if not live(n):
+            if not live(n) or (n, g) in made:
                 return
+            made.add((n, g))
             agr_v, ni = agr_view(n)
             sa_v = sas[(n, g)][:].rearrange("p (t c a e) -> p a c e t", t=4, c=4, a=2)
             for a in range(2):
@@ -148,8 +153,9 @@ def tile_seteq3to3_t_kernel(tc, x, coefs, bias, out):
                     )
 
         def sum_over_i(n):
-            if not live(n):
+            if not live(n) or ("i", n) in made:
                 return
+            made.add(("i", n))
             agr_v, ni = agr_view(n)
             s1 = s1p.tile([P, 2, 2, 256], F32, name="s1")
             for g in range(2):
@@ -163,8 +169,9 @@ def tile_seteq3to3_t_kernel(tc, x, coefs, bias, out):
                 )
 
         def quantise_x(n):
-            if not live(n):
+            if not live(n) or ("q", n) in made:
                 return
+            made.add(("q", n))
             xq = xcd.tile([P, 1024], U32, align_bytes=64, name="xq")
             xs = xcd.tile([P, 1024], U8, align_bytes=64, name="xs")
             for g in range(2):
@@ -334,7 +341,7 @@ def tile_seteq3to3_t_kernel(tc, x, coefs, bias, out):
             mains[(n, m)] = mps
 
         def back_finish(late, bp1, bp2, n):
-            osb = late.tile([P, 2, 512], F32, name="osb")
+            osb = bp2.tile([P, 2, 512], F32, name="osb", tag="osb")
             for m in range(2):
                 p0b, p1b, p2b = spread(n, m)
                 b2 = bbs[n][m]
@@ -425,6 +432,11 @@ def tile_seteq3to3_t_kernel(tc, x, coefs, bias, out):
             sums_out(m, 1)
             for nb, mb in todo[2:]:
                 main_product(nb, mb)
+            if n == NBATCH - 1:
+                for g in range(2):
+                    sums(n, g, 0)
+                    sums(n, g, 1)
+                    sums_out(n, g)
             sum_over_i(m)
             regroup(n, "v", (0, 1))
             quantise_x(m)
@@ -439,8 +451,12 @@ def tile_seteq3to3_t_kernel(tc, x, coefs, bias, out):
         def step_b(k, late, bp1, bp2):
             for n in state["now"]:
                 back_finish(late, bp1, bp2, n)
+            if k == NBATCH - 1:
+                sum_over_i(k)
             if k in quant_at:
                 group_quantise(late, quant_at[k])
+            if k == NBATCH - 1:
+                quantise_x(k)
             grp = stage_at.get(k)
             if grp is not None:
                 qsbs = q_products(late, grp)
@@ -459,7 +475,7 @@ def tile_seteq3to3_t_kernel(tc, x, coefs, bias, out):
                     bias_setup()
         late = ctx.enter_context(tc.tile_pool(name="late", bufs=2))
         bp1 = ctx.enter_context(tc.tile_pool(name="bp1", bufs=2))
-        bp2 = ctx.enter_context(tc.tile_pool(name="bp2", bufs=4))
+        bp2 = ctx.enter_context(tc.tile_pool(name="bp2", bufs=BP2))
         step_b(4, late, bp1, bp2)
         for k in range(5, NBATCH + 6):
             step_a(k, None, late)

@@ -40,8 +40,7 @@ def tile_seteq3to3_t_kernel(tc, x, coefs, bias, out):
         s1p = ctx.enter_context(tc.tile_pool(name="s1p", bufs=1))
         agp = ctx.enter_context(tc.tile_pool(name="agp", bufs=2))
         pst = ctx.enter_context(tc.psum_pool(name="pst", bufs=2))
-        psa = ctx.enter_context(tc.psum_pool(name="psa", bufs=1))
-        psv = ctx.enter_context(tc.psum_pool(name="psv", bufs=1))
+        psa = ctx.enter_context(tc.psum_pool(name="psa", bufs=2))
         psx = ctx.enter_context(tc.psum_pool(name="psx", bufs=4))
 
         cq = keep.tile([P, 4 * NB * P], U32, align_bytes=64, name="cq")
@@ -119,21 +118,22 @@ def tile_seteq3to3_t_kernel(tc, x, coefs, bias, out):
             if not live(n) or (n, g, h) in made:
                 return
             made.add((n, g, h))
-            if g == 0 and h == 0:
-                svs[n] = psv.tile([P, 512], F32, name="sv")
             if h == 0:
                 sas[(n, g)] = psa.tile([P, 512], F32, name="sa")
-            sa = sas[(n, g)]
-            sv = svs[n]
+            sa = sas[(n, g)][:, 0:256].bitcast(BF16)
+            sv = sas[(n, g)][:, 256:352]
             for t in (2 * h, 2 * h + 1):
+                with nc.allow_low_precision(reason="each sum is made whole in float32 by one matmul and rounded once to bfloat16"):
+                    for c in range(4):
+                        o = ((g * 4 + t) * 4 + c) * P
+                        nc.tensor.matmul(
+                            out=sa[:, (t * 4 + c) * 32 : (t * 4 + c + 1) * 32],
+                            lhsT=xts[n][:, o : o + P], rhs=sb[:, 0:32], start=True, stop=True,
+                        )
                 for c in range(4):
                     o = ((g * 4 + t) * 4 + c) * P
                     nc.tensor.matmul(
-                        out=sa[:, (t * 4 + c) * 32 : (t * 4 + c + 1) * 32],
-                        lhsT=xts[n][:, o : o + P], rhs=sb[:, 0:32], start=True, stop=True,
-                    )
-                    nc.tensor.matmul(
-                        out=sv[:, (g * 4 + t) * 24 : (g * 4 + t + 1) * 24],
+                        out=sv[:, t * 24 : (t + 1) * 24],
                         lhsT=xts[n][:, o : o + P], rhs=sb[:, 32 + 24 * c : 56 + 24 * c], start=(c == 0), stop=(c == 3),
                     )
 
@@ -142,15 +142,13 @@ def tile_seteq3to3_t_kernel(tc, x, coefs, bias, out):
                 return
             made.add((n, g))
             agr_v, ni = agr_view(n)
-            sa_v = sas[(n, g)][:].rearrange("p (t c a e) -> p a c e t", t=4, c=4, a=2)
+            sa_v = sas[(n, g)][:, 0:256].bitcast(BF16).rearrange("p (t c a e) -> p a c e t", t=4, c=4, a=2)
             for a in range(2):
                 nc.scalar.copy(out=agr_v[:, 1 + a, g, ni].rearrange("p (c e) t -> p c e t", c=4), in_=sa_v[:, a])
-            if g == 1:
-                for gg in range(2):
-                    nc.scalar.copy(
-                        out=vgr_v[:, :, gg, ni * 8 : (ni + 1) * 8, :],
-                        in_=svs[n][:, gg * 96 : (gg + 1) * 96].rearrange("p (t v r) -> p v r t", t=4, v=3),
-                    )
+            nc.scalar.copy(
+                out=vgr_v[:, :, g, ni * 8 : (ni + 1) * 8, :],
+                in_=sas[(n, g)][:, 256:352].rearrange("p (t v r) -> p v r t", t=4, v=3),
+            )
 
         def sum_over_i(n):
             if not live(n) or ("i", n) in made:

@@ -143,8 +143,7 @@ def tile_seteq3to3_t_kernel(tc, x, coefs, bias, out):
             made.add((n, g))
             agr_v, ni = agr_view(n)
             sa_v = sas[(n, g)][:, 0:256].bitcast(BF16).rearrange("p (t c a e) -> p a c e t", t=4, c=4, a=2)
-            for a in range(2):
-                nc.scalar.copy(out=agr_v[:, 1 + a, g, ni].rearrange("p (c e) t -> p c e t", c=4), in_=sa_v[:, a])
+            nc.scalar.copy(out=agr_v[:, 1:3, g, ni].rearrange("p a (c e) t -> p a c e t", c=4), in_=sa_v)
             nc.scalar.copy(
                 out=vgr_v[:, :, g, ni * 8 : (ni + 1) * 8, :],
                 in_=sas[(n, g)][:, 256:352].rearrange("p (t v r) -> p v r t", t=4, v=3),
@@ -161,9 +160,8 @@ def tile_seteq3to3_t_kernel(tc, x, coefs, bias, out):
                     out=s1[:, g], in_=xgs[n][g][:].rearrange("p (h i e) -> p h e i", h=2, i=4), axis=AX, op=ADD
                 )
             with nc.allow_low_precision(reason="the sum is made in float32 and rounded once to bfloat16"):
-                nc.vector.tensor_reduce(
-                    out=agr_v[:, 0, :, ni].rearrange("p g q t -> p g (q t)"),
-                    in_=s1[:].rearrange("p g h e -> p g e h"), axis=AX, op=ADD,
+                nc.vector.tensor_tensor(
+                    out=agr_v[:, 0, :, ni].rearrange("p g q t -> p g (q t)"), in0=s1[:, :, 0], in1=s1[:, :, 1], op=ADD,
                 )
 
         def quantise_x(n):
@@ -363,7 +361,6 @@ def tile_seteq3to3_t_kernel(tc, x, coefs, bias, out):
             nc.sync.dma_start(out=o_v[n], in_=osb[:])
 
         load(0)
-        load(1)
         ident = keep.tile([P, P], BF16, name="ident")
         make_identity(nc, ident[:])
         sf = keep.tile([P, P], F32, name="sf")
@@ -466,6 +463,7 @@ def tile_seteq3to3_t_kernel(tc, x, coefs, bias, out):
 
         with tc.tile_pool(name="cst", bufs=2) as cst:
             cload(cst, 0)
+            load(1)
             cload(cst, 1)
             for k in range(5):
                 step_a(k, cst, None)

@@ -89,11 +89,13 @@ def tile_seteq3to3_t_kernel(tc, x, coefs, bias, out):
             return agrs[grp][:, :, 0 : gn * 512].rearrange("p a (g n q t) -> p a g n q t", g=2, n=gn, t=4), n - n0
 
         def regroup(n, who, halves):
-            if not live(n) or who != ("v" if n < 4 else "s"):
+            if not live(n):
                 return
             if n not in xgs:
                 xgs[n] = []
             for g in halves:
+                if who != ("v" if n < 4 and g == 1 else "s"):
+                    continue
                 xg = xgp.tile([P, 2048], BF16, align_bytes=64, name="xg%d" % g)
                 dst = xg[:].rearrange("p (c i t) -> p c t i", i=4, t=4)
                 src = raws[n][:, g * 2048 : (g + 1) * 2048].rearrange("p (t c i) -> p c t i", t=4, i=4)

@@ -317,7 +317,10 @@ def tile_seteq3to3_t_kernel(tc, x, coefs, bias, out):
                 p0b, p1b, p2b = spread(n, m)
                 on_vector = last and m == 1
                 b2 = None
-                if not on_vector:
+                if not on_vector and n % 2 == 1:
+                    b2 = bp2.tile([P, 512], F32, name="b2")
+                    nc.gpsimd.tensor_tensor(out=b2[:].rearrange("p (i j k) -> p i j k", i=8, j=8), in0=p0b, in1=p1b, op=ADD)
+                elif not on_vector:
                     b1 = bp1.tile([P, 512], F32, name="b1")
                     b2 = bp2.tile([P, 512], F32, name="b2")
                     nc.gpsimd.tensor_tensor(out=b1[:].rearrange("p (i j k) -> p i j k", i=8, j=8), in0=p0b, in1=p1b, op=ADD)
@@ -360,6 +363,12 @@ def tile_seteq3to3_t_kernel(tc, x, coefs, bias, out):
                     )
                 else:
                     nc.vector.tensor_tensor(out=osb[:, m], in0=mps[:], in1=b2[:], op=ADD)
+            for m in range(2):
+                if n % 2 == 1 and bbs[n][m] is not None:
+                    nc.vector.tensor_tensor(
+                        out=osb[:, m].rearrange("p (e k) -> p e k", k=8), in0=osb[:, m].rearrange("p (e k) -> p e k", k=8),
+                        in1=spread(n, m)[2], op=ADD,
+                    )
             nc.sync.dma_start(out=o_v[n], in_=osb[:])
 
         load(0)

@@ -20,6 +20,8 @@ GROUPS = ((0, 4), (4, 4), (8, 4), (12, 2), (14, 2))
 NB = 19
 CHUNKS = ((0, 4, "s"), (4, 8, "g"), (8, 12, "s"), (12, 16, "g"), (16, 19, "v"))
 BP2 = 4
+XV = 2
+PE_A0 = (1, 15)
 FLOPS = 2 * 1024 * 256 * (8192 + 9 * 1024 + 9 * 128)
 
 
@@ -64,6 +66,7 @@ def tile_seteq3to3_t_kernel(tc, x, coefs, bias, out):
         xgs = {}
         xts = {}
         sas = {}
+        a0s = {}
         svs = {}
         agrs = {}
         xqs = {}
@@ -94,7 +97,7 @@ def tile_seteq3to3_t_kernel(tc, x, coefs, bias, out):
             if n not in xgs:
                 xgs[n] = []
             for g in halves:
-                if who != ("v" if n < 4 and g == 1 else "s"):
+                if who != ("v" if n < 1 or (n < XV and g == 1) else "s"):
                     continue
                 xg = xgp.tile([P, 2048], BF16, align_bytes=64, name="xg%d" % g)
                 dst = xg[:].rearrange("p (c i t) -> p c t i", i=4, t=4)
@@ -122,37 +125,55 @@ def tile_seteq3to3_t_kernel(tc, x, coefs, bias, out):
             made.add((n, g, h))
             if h == 0:
                 sas[(n, g)] = psa.tile([P, 512], F32, name="sa")
-            sa = sas[(n, g)][:, 0:256].bitcast(BF16)
-            sv = sas[(n, g)][:, 256:352]
+                if n in PE_A0 and g == 0:
+                    a0s[n] = pst.tile([P, 1024], BF16, name="a0", tag="tp")[:].bitcast(F32) if n == NBATCH - 1 else psx.tile([P, 512], F32, name="a0", tag="mx")[:]
+            sa = sas[(n, g)][:, 0:288].bitcast(BF16)
+            sv = sas[(n, g)][:, 288:352]
             for t in (2 * h, 2 * h + 1):
                 with nc.allow_low_precision(reason="each sum is made whole in float32 by one matmul and rounded once to bfloat16"):
                     for c in range(4):
                         o = ((g * 4 + t) * 4 + c) * P
                         nc.tensor.matmul(
-                            out=sa[:, (t * 4 + c) * 32 : (t * 4 + c + 1) * 32],
-                            lhsT=xts[n][:, o : o + P], rhs=sb[:, 0:32], start=True, stop=True,
+                            out=sa[:, (t * 4 + c) * 36 : (t * 4 + c) * 36 + 34],
+                            lhsT=xts[n][:, o : o + P], rhs=sb[:, 0:34], start=True, stop=True,
                         )
                 for c in range(4):
                     o = ((g * 4 + t) * 4 + c) * P
                     nc.tensor.matmul(
-                        out=sv[:, t * 24 : (t + 1) * 24],
-                        lhsT=xts[n][:, o : o + P], rhs=sb[:, 32 + 24 * c : 56 + 24 * c], start=(c == 0), stop=(c == 3),
+                        out=sv[:, t * 16 : (t + 1) * 16],
+                        lhsT=xts[n][:, o : o + P], rhs=sb[:, 34:50], start=(c == 0), stop=(c == 3),
                     )
+                if n in PE_A0:
+                    for c in range(4):
+                        o = ((g * 4 + t) * 4 + c) * P
+                        nc.tensor.matmul(
+                            out=a0s[n][:, (g * 4 + t) * 64 : (g * 4 + t + 1) * 64],
+                            lhsT=xts[n][:, o : o + P], rhs=sb[:, 64:128], start=(c == 0), stop=(c == 3),
+                        )
 
         def sums_out(n, g):
             if not live(n) or (n, g) in made:
                 return
             made.add((n, g))
             agr_v, ni = agr_view(n)
-            sa_v = sas[(n, g)][:, 0:256].bitcast(BF16).rearrange("p (t c a e) -> p a c e t", t=4, c=4, a=2)
-            nc.scalar.copy(out=agr_v[:, 1:3, g, ni].rearrange("p a (c e) t -> p a c e t", c=4), in_=sa_v)
+            sa_v = sas[(n, g)][:, 0:288].bitcast(BF16).rearrange("p (t c w) -> p t c w", t=4, c=4)
             nc.scalar.copy(
-                out=vgr_v[:, :, g, ni * 8 : (ni + 1) * 8, :],
-                in_=sas[(n, g)][:, 256:352].rearrange("p (t v r) -> p v r t", t=4, v=3),
+                out=agr_v[:, 1:3, g, ni].rearrange("p a (c e) t -> p a c e t", c=4),
+                in_=sa_v[:, :, :, 0:32].rearrange("p t c (a e) -> p a c e t", a=2),
             )
+            cols = slice(ni * 8, (ni + 1) * 8)
+            nc.scalar.copy(
+                out=vgr_v[:, 2, g, cols, :].rearrange("p (c i) t -> p c i t", c=4),
+                in_=sa_v[:, :, :, 32:34].rearrange("p t c i -> p c i t"),
+            )
+            nc.scalar.copy(out=vgr_v[:, 0:2, g, cols, :], in_=sas[(n, g)][:, 288:352].rearrange("p (t v r) -> p v r t", t=4, v=2))
+            if n in PE_A0:
+                nc.scalar.copy(
+                    out=agr_v[:, 0, g, ni], in_=a0s[n][:, g * 256 : (g + 1) * 256].rearrange("p (t q) -> p q t", t=4)
+                )
 
         def sum_over_i(n):
-            if not live(n) or ("i", n) in made:
+            if not live(n) or n in PE_A0 or ("i", n) in made:
                 return
             made.add(("i", n))
             agr_v, ni = agr_view(n)
@@ -161,6 +182,7 @@ def tile_seteq3to3_t_kernel(tc, x, coefs, bias, out):
                 nc.vector.tensor_reduce(
                     out=s1[:, g], in_=xgs[n][g][:].rearrange("p (h i e) -> p h e i", h=2, i=4), axis=AX, op=ADD
                 )
+            quantise_x(n)
             with nc.allow_low_precision(reason="the sum is made in float32 and rounded once to bfloat16"):
                 nc.vector.tensor_tensor(
                     out=agr_v[:, 0, :, ni].rearrange("p g q t -> p g (q t)"), in0=s1[:, :, 0], in1=s1[:, :, 1], op=ADD,
@@ -221,10 +243,9 @@ def tile_seteq3to3_t_kernel(tc, x, coefs, bias, out):
             agr = agrs[grp]
             aq = late.tile([P, 1536], U32, align_bytes=64, name="aq")
             asc = late.tile([P, 1536], U8, align_bytes=64, name="asc")
-            vq = late.tile([P, 768], U32, align_bytes=64, name="vq")
-            vs = late.tile([P, 768], U8, align_bytes=64, name="vs")
-            nc.vector.quantize_mx(out=vq[:, 0:512].bitcast(FP8X4), scales=vs[:, 0:512], in_=vgr[:, 0:2048])
-            nc.vector.quantize_mx(out=vq[:, 512:768].bitcast(FP8X4), scales=vs[:, 512:768], in_=vgr[:, 2048:3072])
+            vq = late.tile([P, 512], U32, align_bytes=64, name="vq")
+            vs = late.tile([P, 512], U8, align_bytes=64, name="vs")
+            nc.vector.quantize_mx(out=vq[:].bitcast(FP8X4), scales=vs[:], in_=vgr[:])
             for a3 in range(3):
                 nc.vector.quantize_mx(
                     out=aq[:, a3 * 512 : a3 * 512 + gn * 128].bitcast(FP8X4),
@@ -257,7 +278,7 @@ def tile_seteq3to3_t_kernel(tc, x, coefs, bias, out):
                     for idx in range(6):
                         a3, g = divmod(idx, 2)
                         w, wsc = cw(g, m, 10 + 3 * a3 + pl)
-                        o = (a3 * 2 + g) * P
+                        o = (a3 * 2 + g) * 64
                         nc.tensor.matmul_mx(
                             out=qps[:, pl * P : (pl + 1) * P], lhsT=w, lhsT_scale=wsc,
                             rhs=vq[:, o : o + P].bitcast(FP8X4), rhs_scale=vs[:, o : o + P],
@@ -381,20 +402,17 @@ def tile_seteq3to3_t_kernel(tc, x, coefs, bias, out):
             in_=ident[:].rearrange("p (i j k) -> p i k j", i=2, j=8), axis=AX, op=ADD,
         )
         nc.vector.tensor_reduce(out=sf[:, 16:32], in_=ident[:].rearrange("p (e k) -> p e k", k=8), axis=AX, op=ADD)
-        for c in range(4):
-            o = 32 + 24 * c
-            nc.vector.tensor_reduce(out=sf[:, o : o + 8], in_=ident[:].rearrange("p (e k) -> p k e", k=8), axis=AX, op=ADD)
-            nc.vector.tensor_reduce(
-                out=sf[:, o + 8 : o + 16], in_=ident[:].rearrange("p (i j k) -> p j i k", i=2, j=8), axis=AXY, op=ADD
-            )
-            nc.vector.tensor_reduce(
-                out=sf[:, o + 16 + 2 * c : o + 18 + 2 * c], in_=ident[:].rearrange("p (i e) -> p i e", i=2), axis=AX, op=ADD
-            )
+        nc.vector.tensor_reduce(out=sf[:, 32:34], in_=ident[:].rearrange("p (i e) -> p i e", i=2), axis=AX, op=ADD)
+        nc.vector.tensor_reduce(out=sf[:, 34:42], in_=ident[:].rearrange("p (e k) -> p k e", k=8), axis=AX, op=ADD)
+        nc.vector.tensor_reduce(
+            out=sf[:, 42:50], in_=ident[:].rearrange("p (i j k) -> p j i k", i=2, j=8), axis=AXY, op=ADD
+        )
+        nc.vector.tensor_reduce(out=sf[:, 64:128], in_=ident[:].rearrange("p (i e) -> p e i", i=2), axis=AX, op=ADD)
         sb = keep.tile([P, P], BF16, name="sb")
         nc.vector.tensor_copy(out=sb[:], in_=sf[:])
-        vgr = keep.tile([P, 3072], BF16, align_bytes=64, name="vgr")
+        vgr = keep.tile([P, 2048], BF16, align_bytes=64, name="vgr")
         nc.vector.memset(vgr[:], 0.0)
-        vgr_v = vgr[:].rearrange("p (v g c t) -> p v g c t", v=3, g=2, t=4)
+        vgr_v = vgr[:, 0:1536].rearrange("p (v g c t) -> p v g c t", v=3, g=2, t=4)
         bz = keep.tile([P, P], BF16, name="bz")
         nc.vector.memset(bz[:], 0.0)
         bias_sb = keep.tile([P, 2], F32, name="bias_sb")
@@ -445,6 +463,8 @@ def tile_seteq3to3_t_kernel(tc, x, coefs, bias, out):
                     sums_out(n, g)
             sum_over_i(m)
             regroup(n, "v", (0, 1))
+            if n == 0:
+                sum_over_i(0)
             quantise_x(m)
             if state["cgr"]:
                 step, tiles = state["cgr"][0]

@@ -182,7 +182,6 @@ def tile_seteq3to3_t_kernel(tc, x, coefs, bias, out):
                 nc.vector.tensor_reduce(
                     out=s1[:, g], in_=xgs[n][g][:].rearrange("p (h i e) -> p h e i", h=2, i=4), axis=AX, op=ADD
                 )
-            quantise_x(n)
             with nc.allow_low_precision(reason="the sum is made in float32 and rounded once to bfloat16"):
                 nc.vector.tensor_tensor(
                     out=agr_v[:, 0, :, ni].rearrange("p g q t -> p g (q t)"), in0=s1[:, :, 0], in1=s1[:, :, 1], op=ADD,

@@ -9,7 +9,6 @@ U32 = mybir.dt.uint32
 U8 = mybir.dt.uint8
 FP8X4 = mybir.dt.float8_e4m3fn_x4
 ADD = mybir.AluOpType.add
-MULT = mybir.AluOpType.mult
 AX = mybir.AxisListType.X
 AXY = mybir.AxisListType.XY
 IDENT = mybir.ActivationFunctionType.Identity
@@ -18,10 +17,9 @@ P = 128
 NBATCH = 16
 GROUPS = ((0, 4), (4, 4), (8, 4), (12, 2), (14, 2))
 NB = 19
-CHUNKS = ((0, 4, "s"), (4, 8, "g"), (8, 12, "s"), (12, 16, "g"), (16, 19, "v"))
-BP2 = 4
-XV = 2
-PE_A0 = (1, 15)
+CHUNKS = ((0, 4, "s"), (4, 8, "w"), (8, 12, "s2"), (12, 16, "v"), (16, 19, "u"))
+XV = 4
+PE_A0 = (3, 15)
 FLOPS = 2 * 1024 * 256 * (8192 + 9 * 1024 + 9 * 128)
 
 
@@ -50,7 +48,6 @@ def tile_seteq3to3_t_kernel(tc, x, coefs, bias, out):
 
         group_of = {}
         stage_at = {}
-        fold_at = {}
         quant_at = {}
         for gi, (n0, gn) in enumerate(GROUPS):
             for n in range(n0, n0 + gn):
@@ -58,7 +55,6 @@ def tile_seteq3to3_t_kernel(tc, x, coefs, bias, out):
             done = n0 + gn - (1 if gi == len(GROUPS) - 1 else 0)
             quant_at[done] = gi
             stage_at[done + 1] = gi
-            fold_at[done + 2] = gi
 
         made = set()
         raws = {}
@@ -67,12 +63,10 @@ def tile_seteq3to3_t_kernel(tc, x, coefs, bias, out):
         xts = {}
         sas = {}
         a0s = {}
-        svs = {}
         agrs = {}
         xqs = {}
         gcodes = {}
         psbs = {}
-        bbs = {}
         mains = {}
 
         def live(n):
@@ -119,17 +113,16 @@ def tile_seteq3to3_t_kernel(tc, x, coefs, bias, out):
                 nc.tensor.transpose(tp[:, r * P : (r + 1) * P], raws[n][:, o : o + P], ident[:])
             nc.scalar.copy(out=xts[n][:, u * 1024 : (u + 1) * 1024], in_=tp[:])
 
-        def sums(n, g, h):
-            if not live(n) or (n, g, h) in made:
+        def sums(n, g):
+            if not live(n) or (n, g) in made:
                 return
-            made.add((n, g, h))
-            if h == 0:
-                sas[(n, g)] = psa.tile([P, 512], F32, name="sa")
-                if n in PE_A0 and g == 0:
-                    a0s[n] = pst.tile([P, 1024], BF16, name="a0", tag="tp")[:].bitcast(F32) if n == NBATCH - 1 else psx.tile([P, 512], F32, name="a0", tag="mx")[:]
+            made.add((n, g))
+            sas[(n, g)] = psa.tile([P, 512], F32, name="sa")
+            if n in PE_A0 and g == 0:
+                a0s[n] = pst.tile([P, 1024], BF16, name="a0", tag="tp")[:].bitcast(F32) if n == NBATCH - 1 else psx.tile([P, 512], F32, name="a0", tag="mx")[:]
             sa = sas[(n, g)][:, 0:288].bitcast(BF16)
             sv = sas[(n, g)][:, 288:352]
-            for t in (2 * h, 2 * h + 1):
+            for t in range(4):
                 with nc.allow_low_precision(reason="each sum is made whole in float32 by one matmul and rounded once to bfloat16"):
                     for c in range(4):
                         o = ((g * 4 + t) * 4 + c) * P
@@ -150,11 +143,6 @@ def tile_seteq3to3_t_kernel(tc, x, coefs, bias, out):
                             out=a0s[n][:, (g * 4 + t) * 64 : (g * 4 + t + 1) * 64],
                             lhsT=xts[n][:, o : o + P], rhs=sb[:, 64:128], start=(c == 0), stop=(c == 3),
                         )
-
-        def sums_out(n, g):
-            if not live(n) or (n, g) in made:
-                return
-            made.add((n, g))
             agr_v, ni = agr_view(n)
             sa_v = sas[(n, g)][:, 0:288].bitcast(BF16).rearrange("p (t c w) -> p t c w", t=4, c=4)
             nc.scalar.copy(
@@ -177,14 +165,16 @@ def tile_seteq3to3_t_kernel(tc, x, coefs, bias, out):
                 return
             made.add(("i", n))
             agr_v, ni = agr_view(n)
-            s1 = s1p.tile([P, 2, 2, 256], F32, name="s1")
+            r1 = s1p.tile([P, 2, 1024], F32, name="r1")
+            r2 = s1p.tile([P, 2, 512], F32, name="r2")
             for g in range(2):
-                nc.vector.tensor_reduce(
-                    out=s1[:, g], in_=xgs[n][g][:].rearrange("p (h i e) -> p h e i", h=2, i=4), axis=AX, op=ADD
-                )
+                nc.vector.tensor_tensor(out=r1[:, g], in0=xgs[n][g][:, 0:1024], in1=xgs[n][g][:, 1024:2048], op=ADD)
+            for g in range(2):
+                nc.vector.tensor_tensor(out=r2[:, g], in0=r1[:, g, 0:512], in1=r1[:, g, 512:1024], op=ADD)
+            quantise_x(n)
             with nc.allow_low_precision(reason="the sum is made in float32 and rounded once to bfloat16"):
                 nc.vector.tensor_tensor(
-                    out=agr_v[:, 0, :, ni].rearrange("p g q t -> p g (q t)"), in0=s1[:, :, 0], in1=s1[:, :, 1], op=ADD,
+                    out=agr_v[:, 0, :, ni].rearrange("p g q t -> p g (q t)"), in0=r2[:, :, 0:256], in1=r2[:, :, 256:512], op=ADD,
                 )
 
         def quantise_x(n):
@@ -210,12 +200,10 @@ def tile_seteq3to3_t_kernel(tc, x, coefs, bias, out):
             src = craws[step][:].rearrange("p t (s b) -> p s t b", b=NB)
             tiles = []
             for b0, b1, who in CHUNKS:
-                cgr = cst.tile([P, 2048], BF16, align_bytes=64, name="cgr_" + who)
+                cgr = cst.tile([P, 2048], BF16, align_bytes=64, name="cgr", bufs=6)
                 dst = cgr[:, 0 : (b1 - b0) * 512].rearrange("p (b s t) -> p s t b", b=b1 - b0, t=4)
-                if who == "s":
+                if who[0] == "s":
                     nc.scalar.copy(out=dst, in_=src[:, :, :, b0:b1])
-                elif who == "g":
-                    nc.gpsimd.tensor_scalar(out=dst, in0=src[:, :, :, b0:b1], scalar1=1.0, scalar2=0.0, op0=MULT, op1=ADD)
                 else:
                     nc.vector.tensor_copy(out=dst, in_=src[:, :, :, b0:b1])
                 tiles.append(cgr)
@@ -224,7 +212,7 @@ def tile_seteq3to3_t_kernel(tc, x, coefs, bias, out):
         def coef_quantise(step, tiles):
             m, g = divmod(step, 2)
             base = (g * 2 + m) * NB * P
-            for (b0, b1, who), cgr in zip(CHUNKS, tiles):
+            for (b0, b1, who), cgr in sorted(zip(CHUNKS, tiles), key=lambda z: z[0][2][0] == "s"):
                 pieces = ((0, 4),) if b1 - b0 == 4 else ((0, 2), (2, 3))
                 for q0, q1 in pieces:
                     nc.vector.quantize_mx(
@@ -291,34 +279,34 @@ def tile_seteq3to3_t_kernel(tc, x, coefs, bias, out):
 
         def p_products(late, grp, m, qsb):
             nw = GROUPS[grp][1] * 64
-            if m >= 0:
-                p10 = late.tile([P, 2, 256], F32, name="p10_%d" % m)
-                p2 = late.tile([P, 256], F32, name="p2_%d" % m)
-                pps = psx.tile([P, 512], F32, name="pps", tag="mx")
-                a_group(pps[:, 0:nw], grp, m, 1)
-                a_group(pps[:, 256 : 256 + nw], grp, m, 0)
-                pp2 = psx.tile([P, 512], F32, name="pp2", tag="mx")
-                a_group(pp2[:, 0:nw], grp, m, 2)
-                nc.scalar.activation(out=p2[:, 0:nw], in_=pp2[:, 0:nw], func=IDENT, bias=bias_sb[:, m : m + 1])
-                psbs[(grp, m)] = (p10, p2)
+            p10 = late.tile([P, 2, 256], F32, name="p10_%d" % m, bufs=2)
+            p2 = late.tile([P, 256], F32, name="p2_%d" % m, bufs=2)
+            pps = psx.tile([P, 512], F32, name="pps", tag="mx")
+            a_group(pps[:, 0:nw], grp, m, 1)
+            a_group(pps[:, 256 : 256 + nw], grp, m, 0)
+            pp2 = psx.tile([P, 512], F32, name="pp2", tag="mx")
+            a_group(pp2[:, 0:nw], grp, m, 2)
+            nc.scalar.activation(out=p2[:, 0:nw], in_=pp2[:, 0:nw], func=IDENT, bias=bias_sb[:, m : m + 1])
+            psbs[(grp, m)] = (p10, p2)
             return (pps, qsb, p10)
 
-        def fold(grp, item):
+        def fold(grp, pair):
             gn = GROUPS[grp][1]
             nw = gn * 64
-            pps, qsb, p10 = item
-            nc.vector.tensor_tensor(
-                out=p10[:, :, 0:nw].rearrange("p l (e k) -> p l e k", k=8),
-                in0=pps[:].rearrange("p (l c) -> p l c", l=2)[:, :, 0:nw].rearrange("p l (e k) -> p l e k", k=8),
-                in1=qsb[:, 0:2, 0 : gn * 8].unsqueeze(3).to_broadcast([P, 2, gn * 8, 8]),
-                op=ADD,
-            )
-            nc.gpsimd.tensor_tensor(
-                out=p10[:, 1, 0:nw].rearrange("p (n j k) -> p n j k", n=gn, k=8),
-                in0=p10[:, 1, 0:nw].rearrange("p (n j k) -> p n j k", n=gn, k=8),
-                in1=qsb[:, 2, 0 : gn * 8].rearrange("p (n k) -> p n k", n=gn).unsqueeze(2).to_broadcast([P, gn, 8, 8]),
-                op=ADD,
-            )
+            for pps, qsb, p10 in pair:
+                nc.vector.tensor_tensor(
+                    out=p10[:, :, 0:nw].rearrange("p l (e k) -> p l e k", k=8),
+                    in0=pps[:].rearrange("p (l c) -> p l c", l=2)[:, :, 0:nw].rearrange("p l (e k) -> p l e k", k=8),
+                    in1=qsb[:, 0:2, 0 : gn * 8].unsqueeze(3).to_broadcast([P, 2, gn * 8, 8]),
+                    op=ADD,
+                )
+            for pps, qsb, p10 in pair:
+                nc.vector.tensor_tensor(
+                    out=p10[:, 1, 0:nw].rearrange("p (n j k) -> p n j k", n=gn, k=8),
+                    in0=p10[:, 1, 0:nw].rearrange("p (n j k) -> p n j k", n=gn, k=8),
+                    in1=qsb[:, 2, 0 : gn * 8].rearrange("p (n k) -> p n k", n=gn).unsqueeze(2).to_broadcast([P, gn, 8, 8]),
+                    op=ADD,
+                )
 
         def spread(n, m):
             grp = group_of[n]
@@ -329,25 +317,6 @@ def tile_seteq3to3_t_kernel(tc, x, coefs, bias, out):
             p1b = p10[:, 0, sl].rearrange("p (i k) -> p i k", i=8).unsqueeze(2).to_broadcast([P, 8, 8, 8])
             p2b = p2[:, sl].unsqueeze(2).to_broadcast([P, 64, 8])
             return p0b, p1b, p2b
-
-        def back_gpsimd(bp1, bp2, n):
-            last = group_of[n] == len(GROUPS) - 1
-            bbs[n] = []
-            for m in range(2):
-                p0b, p1b, p2b = spread(n, m)
-                on_vector = last and m == 1
-                b2 = None
-                if not on_vector and n % 2 == 1:
-                    b2 = bp2.tile([P, 512], F32, name="b2")
-                    nc.gpsimd.tensor_tensor(out=b2[:].rearrange("p (i j k) -> p i j k", i=8, j=8), in0=p0b, in1=p1b, op=ADD)
-                elif not on_vector:
-                    b1 = bp1.tile([P, 512], F32, name="b1")
-                    b2 = bp2.tile([P, 512], F32, name="b2")
-                    nc.gpsimd.tensor_tensor(out=b1[:].rearrange("p (i j k) -> p i j k", i=8, j=8), in0=p0b, in1=p1b, op=ADD)
-                    nc.gpsimd.tensor_tensor(
-                        out=b2[:].rearrange("p (e k) -> p e k", k=8), in0=b1[:].rearrange("p (e k) -> p e k", k=8), in1=p2b, op=ADD
-                    )
-                bbs[n].append(b2)
 
         def main_product(n, m):
             xq, xs = xqs[n]
@@ -361,34 +330,24 @@ def tile_seteq3to3_t_kernel(tc, x, coefs, bias, out):
                 )
             mains[(n, m)] = mps
 
-        def back_finish(late, bp1, bp2, n):
-            osb = bp2.tile([P, 2, 512], F32, name="osb", tag="osb")
-            for m in range(2):
-                p0b, p1b, p2b = spread(n, m)
-                b2 = bbs[n][m]
-                mps = mains[(n, m)]
-                if b2 is None:
-                    b1 = bp1.tile([P, 512], F32, name="b1")
-                    b2 = bp2.tile([P, 512], F32, name="b2")
-                    nc.vector.tensor_tensor(
-                        out=b1[:].rearrange("p (i j k) -> p i j k", i=8, j=8),
-                        in0=mps[:].rearrange("p (i j k) -> p i j k", i=8, j=8), in1=p0b, op=ADD,
-                    )
-                    nc.vector.tensor_tensor(
-                        out=b2[:].rearrange("p (i j k) -> p i j k", i=8, j=8),
-                        in0=b1[:].rearrange("p (i j k) -> p i j k", i=8, j=8), in1=p1b, op=ADD,
-                    )
-                    nc.vector.tensor_tensor(
-                        out=osb[:, m].rearrange("p (e k) -> p e k", k=8), in0=b2[:].rearrange("p (e k) -> p e k", k=8), in1=p2b, op=ADD
-                    )
-                else:
-                    nc.vector.tensor_tensor(out=osb[:, m], in0=mps[:], in1=b2[:], op=ADD)
-            for m in range(2):
-                if n % 2 == 1 and bbs[n][m] is not None:
-                    nc.vector.tensor_tensor(
-                        out=osb[:, m].rearrange("p (e k) -> p e k", k=8), in0=osb[:, m].rearrange("p (e k) -> p e k", k=8),
-                        in1=spread(n, m)[2], op=ADD,
-                    )
+        def back_finish(bp2, n):
+            osb = bp2.tile([P, 2, 512], F32, name="osb")
+            ms = range(2)
+            for m in ms:
+                nc.vector.tensor_tensor(
+                    out=osb[:, m].rearrange("p (i j k) -> p i j k", i=8, j=8),
+                    in0=mains[(n, m)][:].rearrange("p (i j k) -> p i j k", i=8, j=8), in1=spread(n, m)[0], op=ADD,
+                )
+            for m in ms:
+                nc.vector.tensor_tensor(
+                    out=osb[:, m].rearrange("p (i j k) -> p i j k", i=8, j=8),
+                    in0=osb[:, m].rearrange("p (i j k) -> p i j k", i=8, j=8), in1=spread(n, m)[1], op=ADD,
+                )
+            for m in ms:
+                nc.vector.tensor_tensor(
+                    out=osb[:, m].rearrange("p (e k) -> p e k", k=8),
+                    in0=osb[:, m].rearrange("p (e k) -> p e k", k=8), in1=spread(n, m)[2], op=ADD,
+                )
             nc.sync.dma_start(out=o_v[n], in_=osb[:])
 
         load(0)
@@ -416,93 +375,81 @@ def tile_seteq3to3_t_kernel(tc, x, coefs, bias, out):
         nc.vector.memset(bz[:], 0.0)
         bias_sb = keep.tile([P, 2], F32, name="bias_sb")
 
+        nc.sync.dma_start(out=bz[0:2, :], in_=b_v)
+
         def bias_setup():
-            nc.sync.dma_start(out=bz[0:2, :], in_=b_v)
             bps = pst.tile([P, 1024], BF16, name="bps", tag="tp")
             nc.tensor.transpose(bps[:, 0:P], bz[:], ident[:])
             nc.vector.tensor_copy(out=bias_sb[:], in_=bps[:, 0:2])
 
-        state = {"folds": {}, "cgr": [], "to_g": [], "to_f": [], "now": []}
+        state = {"cgr": [], "ready": [], "products": None}
 
-        def step_a(k, cst, late):
+        def step(k, cst, late, fin):
             n = k
             m = k - 1
+            last = n == NBATCH - 1
             load(k + 2)
-            grp = fold_at.get(k)
-            if grp is not None:
-                for item in state["folds"][grp]:
-                    fold(grp, item)
+            if state["products"] is not None:
+                grp, pair = state["products"]
+                state["products"] = None
+                fold(grp, pair)
                 n0, gn = GROUPS[grp]
-                state["to_g"] = state["to_g"] + list(range(n0, n0 + gn))
-            state["now"] = state["to_f"][0:2]
-            state["to_f"] = state["to_f"][2:]
-            todo = [(nb, mb) for nb in state["now"] for mb in range(2)]
-            if todo:
-                main_product(todo[0][0], todo[0][1])
+                state["ready"] = state["ready"] + list(range(n0, n0 + gn))
+            now = state["ready"][0:2]
+            state["ready"] = state["ready"][2:]
+            todo = [(nb, mb) for nb in now for mb in range(2)]
+            for nb, mb in todo[0:1]:
+                main_product(nb, mb)
             transposes(n, 0)
             transposes(n, 1)
             regroup(n, "s", (0,))
-            sums(m, 0, 0)
-            sums(m, 0, 1)
-            sums_out(m, 0)
-            if len(todo) > 1:
-                main_product(todo[1][0], todo[1][1])
+            sums(m, 0)
+            for nb, mb in todo[1:2]:
+                main_product(nb, mb)
             transposes(n, 2)
             transposes(n, 3)
             regroup(n, "s", (1,))
-            sums(m, 1, 0)
-            sums(m, 1, 1)
-            sums_out(m, 1)
+            sums(m, 1)
             for nb, mb in todo[2:]:
                 main_product(nb, mb)
-            if n == NBATCH - 1:
-                for g in range(2):
-                    sums(n, g, 0)
-                    sums(n, g, 1)
-                    sums_out(n, g)
+            if last:
+                sums(n, 0)
+                sums(n, 1)
             sum_over_i(m)
             regroup(n, "v", (0, 1))
             if n == 0:
-                sum_over_i(0)
+                sum_over_i(n)
             quantise_x(m)
             if state["cgr"]:
-                step, tiles = state["cgr"][0]
+                coef_quantise(k - 1, state["cgr"])
                 state["cgr"] = []
-                coef_quantise(step, tiles)
             if k < 4:
-                state["cgr"] = [(k, coef_regroup(cst, k))]
+                state["cgr"] = coef_regroup(cst, k)
                 cload(cst, k + 2)
-
-        def step_b(k, late, bp1, bp2):
-            for n in state["now"]:
-                back_finish(late, bp1, bp2, n)
-            if k == NBATCH - 1:
-                sum_over_i(k)
+            for nb in now:
+                back_finish(fin, nb)
+            if last:
+                sum_over_i(n)
             if k in quant_at:
                 group_quantise(late, quant_at[k])
-            if k == NBATCH - 1:
-                quantise_x(k)
+            if last:
+                quantise_x(n)
             grp = stage_at.get(k)
             if grp is not None:
                 qsbs = q_products(late, grp)
-                state["folds"][grp] = [p_products(late, grp, mb, qsbs[mb]) for mb in range(2)]
-            for n in state["to_g"][0:2]:
-                back_gpsimd(bp1, bp2, n)
-                state["to_f"] = state["to_f"] + [n]
-            state["to_g"] = state["to_g"][2:]
+                state["products"] = (grp, [p_products(late, grp, mb, qsbs[mb]) for mb in range(2)])
 
         with tc.tile_pool(name="cst", bufs=2) as cst:
             cload(cst, 0)
             load(1)
             cload(cst, 1)
-            for k in range(5):
-                step_a(k, cst, None)
-                if k == 2:
+            for k in range(4):
+                step(k, cst, None, None)
+                if k == 0:
                     bias_setup()
+            coef_quantise(3, state["cgr"])
+            state["cgr"] = []
         late = ctx.enter_context(tc.tile_pool(name="late", bufs=2))
-        bp1 = ctx.enter_context(tc.tile_pool(name="bp1", bufs=2))
-        bp2 = ctx.enter_context(tc.tile_pool(name="bp2", bufs=BP2))
-        step_b(4, late, bp1, bp2)
-        for k in range(5, NBATCH + 6):
-            step_a(k, None, late)
-            step_b(k, late, bp1, bp2)
+        fin = ctx.enter_context(tc.tile_pool(name="fin", bufs=4))
+        for k in range(4, NBATCH + 6):
+            step(k, None, late, fin)

@@ -18,7 +18,7 @@ NBATCH = 16
 GROUPS = ((0, 4), (4, 4), (8, 4), (12, 2), (14, 2))
 NB = 19
 CHUNKS = ((0, 4, "s"), (4, 8, "w"), (8, 12, "s2"), (12, 16, "v"), (16, 19, "u"))
-XV = 4
+XV = 5
 PE_A0 = (3, 15)
 FLOPS = 2 * 1024 * 256 * (8192 + 9 * 1024 + 9 * 128)
 
@@ -67,7 +67,10 @@ def tile_seteq3to3_t_kernel(tc, x, coefs, bias, out):
         xqs = {}
         gcodes = {}
         psbs = {}
+        qsbs = {}
+        pss = {}
         mains = {}
+        pre = {}
 
         def live(n):
             return 0 <= n < NBATCH
@@ -257,7 +260,6 @@ def tile_seteq3to3_t_kernel(tc, x, coefs, bias, out):
         def q_products(late, grp):
             gn = GROUPS[grp][1]
             aq, asc, vq, vs = gcodes[grp]
-            qsbs = []
             for m in range(2):
                 qsb = late.tile([P, 3, 32], F32, name="qsb%d" % m)
                 qps = psx.tile([P, 512], F32, name="qps", tag="mx")
@@ -274,37 +276,41 @@ def tile_seteq3to3_t_kernel(tc, x, coefs, bias, out):
                 nc.scalar.copy(
                     out=qsb[:, :, 0 : gn * 8], in_=qps[:, 0:384].rearrange("p (l c) -> p l c", l=3)[:, :, 0 : gn * 8]
                 )
-                qsbs.append(qsb)
-            return qsbs
+                qsbs[(grp, m)] = qsb
 
-        def p_products(late, grp, m, qsb):
+        def p_products(late, grp, m):
             nw = GROUPS[grp][1] * 64
-            p10 = late.tile([P, 2, 256], F32, name="p10_%d" % m, bufs=2)
-            p2 = late.tile([P, 256], F32, name="p2_%d" % m, bufs=2)
+            p10 = late.tile([P, 2, 256], F32, name="p10_%d" % m)
+            p2 = late.tile([P, 256], F32, name="p2_%d" % m)
             pps = psx.tile([P, 512], F32, name="pps", tag="mx")
             a_group(pps[:, 0:nw], grp, m, 1)
             a_group(pps[:, 256 : 256 + nw], grp, m, 0)
             pp2 = psx.tile([P, 512], F32, name="pp2", tag="mx")
             a_group(pp2[:, 0:nw], grp, m, 2)
-            nc.scalar.activation(out=p2[:, 0:nw], in_=pp2[:, 0:nw], func=IDENT, bias=bias_sb[:, m : m + 1])
             psbs[(grp, m)] = (p10, p2)
-            return (pps, qsb, p10)
+            pss[(grp, m)] = (pps, pp2)
 
-        def fold(grp, pair):
+        def p2_out(grp, m):
+            nw = GROUPS[grp][1] * 64
+            nc.scalar.activation(
+                out=psbs[(grp, m)][1][:, 0:nw], in_=pss[(grp, m)][1][:, 0:nw], func=IDENT, bias=bias_sb[:, m : m + 1]
+            )
+
+        def fold(grp):
             gn = GROUPS[grp][1]
             nw = gn * 64
-            for pps, qsb, p10 in pair:
+            for m in range(2):
                 nc.vector.tensor_tensor(
-                    out=p10[:, :, 0:nw].rearrange("p l (e k) -> p l e k", k=8),
-                    in0=pps[:].rearrange("p (l c) -> p l c", l=2)[:, :, 0:nw].rearrange("p l (e k) -> p l e k", k=8),
-                    in1=qsb[:, 0:2, 0 : gn * 8].unsqueeze(3).to_broadcast([P, 2, gn * 8, 8]),
+                    out=psbs[(grp, m)][0][:, :, 0:nw].rearrange("p l (e k) -> p l e k", k=8),
+                    in0=pss[(grp, m)][0][:].rearrange("p (l c) -> p l c", l=2)[:, :, 0:nw].rearrange("p l (e k) -> p l e k", k=8),
+                    in1=qsbs[(grp, m)][:, 0:2, 0 : gn * 8].unsqueeze(3).to_broadcast([P, 2, gn * 8, 8]),
                     op=ADD,
                 )
-            for pps, qsb, p10 in pair:
+            for m in range(2):
+                p0 = psbs[(grp, m)][0][:, 1, 0:nw].rearrange("p (n j k) -> p n j k", n=gn, k=8)
                 nc.vector.tensor_tensor(
-                    out=p10[:, 1, 0:nw].rearrange("p (n j k) -> p n j k", n=gn, k=8),
-                    in0=p10[:, 1, 0:nw].rearrange("p (n j k) -> p n j k", n=gn, k=8),
-                    in1=qsb[:, 2, 0 : gn * 8].rearrange("p (n k) -> p n k", n=gn).unsqueeze(2).to_broadcast([P, gn, 8, 8]),
+                    out=p0, in0=p0,
+                    in1=qsbs[(grp, m)][:, 2, 0 : gn * 8].rearrange("p (n k) -> p n k", n=gn).unsqueeze(2).to_broadcast([P, gn, 8, 8]),
                     op=ADD,
                 )
 
@@ -330,27 +336,41 @@ def tile_seteq3to3_t_kernel(tc, x, coefs, bias, out):
                 )
             mains[(n, m)] = mps
 
-        def back_finish(bp2, n):
-            osb = bp2.tile([P, 2, 512], F32, name="osb")
-            ms = range(2)
-            for m in ms:
-                nc.vector.tensor_tensor(
-                    out=osb[:, m].rearrange("p (i j k) -> p i j k", i=8, j=8),
-                    in0=mains[(n, m)][:].rearrange("p (i j k) -> p i j k", i=8, j=8), in1=spread(n, m)[0], op=ADD,
-                )
-            for m in ms:
-                nc.vector.tensor_tensor(
-                    out=osb[:, m].rearrange("p (i j k) -> p i j k", i=8, j=8),
-                    in0=osb[:, m].rearrange("p (i j k) -> p i j k", i=8, j=8), in1=spread(n, m)[1], op=ADD,
-                )
-            for m in ms:
-                nc.vector.tensor_tensor(
-                    out=osb[:, m].rearrange("p (e k) -> p e k", k=8),
-                    in0=osb[:, m].rearrange("p (e k) -> p e k", k=8), in1=spread(n, m)[2], op=ADD,
-                )
-            nc.sync.dma_start(out=o_v[n], in_=osb[:])
+        def prepare(fin, n):
+            n0, gn = GROUPS[group_of[n]]
+            for m in range(2):
+                if 2 * (n - n0) + m > gn:
+                    b = fin.tile([P, 512], F32, name="b")
+                    p0b, p1b, p2b = spread(n, m)
+                    nc.gpsimd.tensor_tensor(out=b[:].rearrange("p (i j k) -> p i j k", i=8, j=8), in0=p0b, in1=p1b, op=ADD)
+                    pre[(n, m)] = b
+
+        def finish(fin, n):
+            osb = fin.tile([P, 2, 512], F32, name="osb")
+            for m in range(2):
+                if (n, m) in pre:
+                    nc.vector.tensor_tensor(out=osb[:, m], in0=mains[(n, m)][:], in1=pre[(n, m)][:], op=ADD)
+                else:
+                    nc.vector.tensor_tensor(
+                        out=osb[:, m].rearrange("p (i j k) -> p i j k", i=8, j=8),
+                        in0=mains[(n, m)][:].rearrange("p (i j k) -> p i j k", i=8, j=8), in1=spread(n, m)[0], op=ADD,
+                    )
+            for m in range(2):
+                if (n, m) not in pre:
+                    o = osb[:, m].rearrange("p (i j k) -> p i j k", i=8, j=8)
+                    nc.vector.tensor_tensor(out=o, in0=o, in1=spread(n, m)[1], op=ADD)
+            for m in range(2):
+                o = osb[:, m].rearrange("p (e k) -> p e k", k=8)
+                nc.vector.tensor_tensor(out=o, in0=o, in1=spread(n, m)[2], op=ADD)
+                if n == NBATCH - 1:
+                    nc.sync.dma_start(out=o_v[n][:, m], in_=osb[:, m])
+            if n < NBATCH - 1:
+                nc.sync.dma_start(out=o_v[n], in_=osb[:])
 
         load(0)
+        bz = keep.tile([P, P], BF16, name="bz")
+        nc.vector.memset(bz[:], 0.0)
+        nc.sync.dma_start(out=bz[0:2, :], in_=b_v)
         ident = keep.tile([P, P], BF16, name="ident")
         make_identity(nc, ident[:])
         sf = keep.tile([P, P], F32, name="sf")
@@ -371,30 +391,40 @@ def tile_seteq3to3_t_kernel(tc, x, coefs, bias, out):
         vgr = keep.tile([P, 2048], BF16, align_bytes=64, name="vgr")
         nc.vector.memset(vgr[:], 0.0)
         vgr_v = vgr[:, 0:1536].rearrange("p (v g c t) -> p v g c t", v=3, g=2, t=4)
-        bz = keep.tile([P, P], BF16, name="bz")
-        nc.vector.memset(bz[:], 0.0)
         bias_sb = keep.tile([P, 2], F32, name="bias_sb")
-
-        nc.sync.dma_start(out=bz[0:2, :], in_=b_v)
 
         def bias_setup():
             bps = pst.tile([P, 1024], BF16, name="bps", tag="tp")
             nc.tensor.transpose(bps[:, 0:P], bz[:], ident[:])
-            nc.vector.tensor_copy(out=bias_sb[:], in_=bps[:, 0:2])
+            nc.scalar.copy(out=bias_sb[:], in_=bps[:, 0:2])
 
-        state = {"cgr": [], "ready": [], "products": None}
+        state = {"cgr": [], "ready": [], "half": None, "whole": None}
+
+        def open_group(grp, fin):
+            fold(grp)
+            n0, gn = GROUPS[grp]
+            for n in range(n0, n0 + gn):
+                prepare(fin, n)
+            state["ready"] = state["ready"] + list(range(n0, n0 + gn))
 
         def step(k, cst, late, fin):
             n = k
             m = k - 1
             last = n == NBATCH - 1
             load(k + 2)
-            if state["products"] is not None:
-                grp, pair = state["products"]
-                state["products"] = None
-                fold(grp, pair)
-                n0, gn = GROUPS[grp]
-                state["ready"] = state["ready"] + list(range(n0, n0 + gn))
+            grp = stage_at.get(k)
+            behind = state["half"]
+            state["half"] = None
+            if behind is not None:
+                regroup(n, "s", (0,))
+                p2_out(behind, 0)
+                p_products(late, behind, 1)
+                regroup(n, "s", (1,))
+                p2_out(behind, 1)
+                open_group(behind, fin)
+            if state["whole"] is not None:
+                open_group(state["whole"], fin)
+                state["whole"] = None
             now = state["ready"][0:2]
             state["ready"] = state["ready"][2:]
             todo = [(nb, mb) for nb in now for mb in range(2)]
@@ -402,16 +432,20 @@ def tile_seteq3to3_t_kernel(tc, x, coefs, bias, out):
                 main_product(nb, mb)
             transposes(n, 0)
             transposes(n, 1)
-            regroup(n, "s", (0,))
+            if behind is None:
+                regroup(n, "s", (0,))
             sums(m, 0)
             for nb, mb in todo[1:2]:
                 main_product(nb, mb)
             transposes(n, 2)
             transposes(n, 3)
-            regroup(n, "s", (1,))
+            if behind is None and (grp is None or last):
+                regroup(n, "s", (1,))
             sums(m, 1)
             for nb, mb in todo[2:]:
                 main_product(nb, mb)
+            if grp is not None and not last:
+                regroup(n, "s", (1,))
             if last:
                 sums(n, 0)
                 sums(n, 1)
@@ -427,17 +461,23 @@ def tile_seteq3to3_t_kernel(tc, x, coefs, bias, out):
                 state["cgr"] = coef_regroup(cst, k)
                 cload(cst, k + 2)
             for nb in now:
-                back_finish(fin, nb)
+                finish(fin, nb)
             if last:
                 sum_over_i(n)
             if k in quant_at:
                 group_quantise(late, quant_at[k])
             if last:
                 quantise_x(n)
-            grp = stage_at.get(k)
             if grp is not None:
-                qsbs = q_products(late, grp)
-                state["products"] = (grp, [p_products(late, grp, mb, qsbs[mb]) for mb in range(2)])
+                q_products(late, grp)
+                p_products(late, grp, 0)
+                if n < NBATCH - 1:
+                    state["half"] = grp
+                else:
+                    p2_out(grp, 0)
+                    p_products(late, grp, 1)
+                    p2_out(grp, 1)
+                    state["whole"] = grp
 
         with tc.tile_pool(name="cst", bufs=2) as cst:
             cload(cst, 0)
@@ -450,6 +490,6 @@ def tile_seteq3to3_t_kernel(tc, x, coefs, bias, out):
             coef_quantise(3, state["cgr"])
             state["cgr"] = []
         late = ctx.enter_context(tc.tile_pool(name="late", bufs=2))
-        fin = ctx.enter_context(tc.tile_pool(name="fin", bufs=4))
+        fin = ctx.enter_context(tc.tile_pool(name="fin", bufs=3))
         for k in range(4, NBATCH + 6):
             step(k, None, late, fin)

@@ -19,6 +19,7 @@ GROUPS = ((0, 4), (4, 4), (8, 4), (12, 2), (14, 2))
 NB = 19
 CHUNKS = ((0, 4, "s"), (4, 8, "w"), (8, 12, "s2"), (12, 16, "v"), (16, 19, "u"))
 XV = 5
+LATE_MAIN = 12
 PE_A0 = (3, 15)
 FLOPS = 2 * 1024 * 256 * (8192 + 9 * 1024 + 9 * 128)
 
@@ -71,6 +72,7 @@ def tile_seteq3to3_t_kernel(tc, x, coefs, bias, out):
         pss = {}
         mains = {}
         pre = {}
+        r2s = {}
 
         def live(n):
             return 0 <= n < NBATCH
@@ -78,7 +80,11 @@ def tile_seteq3to3_t_kernel(tc, x, coefs, bias, out):
         def load(n):
             if live(n):
                 raw = xin.tile([P, 4096], BF16, name="raw")
-                nc.sync.dma_start(out=raw[:].rearrange("p (g w) -> p g w", g=2), in_=x_v[n])
+                if n == 0:
+                    for g in range(2):
+                        nc.sync.dma_start(out=raw[:, g * 2048 : (g + 1) * 2048], in_=x_v[n][:, g])
+                else:
+                    nc.sync.dma_start(out=raw[:].rearrange("p (g w) -> p g w", g=2), in_=x_v[n])
                 raws[n] = raw
 
         def agr_view(n):
@@ -167,14 +173,20 @@ def tile_seteq3to3_t_kernel(tc, x, coefs, bias, out):
             if not live(n) or n in PE_A0 or ("i", n) in made:
                 return
             made.add(("i", n))
-            agr_v, ni = agr_view(n)
             r1 = s1p.tile([P, 2, 1024], F32, name="r1")
             r2 = s1p.tile([P, 2, 512], F32, name="r2")
             for g in range(2):
                 nc.vector.tensor_tensor(out=r1[:, g], in0=xgs[n][g][:, 0:1024], in1=xgs[n][g][:, 1024:2048], op=ADD)
             for g in range(2):
                 nc.vector.tensor_tensor(out=r2[:, g], in0=r1[:, g, 0:512], in1=r1[:, g, 512:1024], op=ADD)
-            quantise_x(n)
+            r2s[n] = r2
+
+        def sum_over_i_end(n):
+            if n not in r2s or ("e", n) in made:
+                return
+            made.add(("e", n))
+            agr_v, ni = agr_view(n)
+            r2 = r2s[n]
             with nc.allow_low_precision(reason="the sum is made in float32 and rounded once to bfloat16"):
                 nc.vector.tensor_tensor(
                     out=agr_v[:, 0, :, ni].rearrange("p g q t -> p g (q t)"), in0=r2[:, :, 0:256], in1=r2[:, :, 256:512], op=ADD,
@@ -306,6 +318,10 @@ def tile_seteq3to3_t_kernel(tc, x, coefs, bias, out):
                     in1=qsbs[(grp, m)][:, 0:2, 0 : gn * 8].unsqueeze(3).to_broadcast([P, 2, gn * 8, 8]),
                     op=ADD,
                 )
+
+        def fold_end(grp):
+            gn = GROUPS[grp][1]
+            nw = gn * 64
             for m in range(2):
                 p0 = psbs[(grp, m)][0][:, 1, 0:nw].rearrange("p (n j k) -> p n j k", n=gn, k=8)
                 nc.vector.tensor_tensor(
@@ -326,7 +342,12 @@ def tile_seteq3to3_t_kernel(tc, x, coefs, bias, out):
 
         def main_product(n, m):
             xq, xs = xqs[n]
-            mps = psx.tile([P, 512], F32, name="mps", tag="mx")
+            if n < LATE_MAIN:
+                mps = psx.tile([P, 512], F32, name="mps", tag="mx")
+            elif n % 2 == 0:
+                mps = pst.tile([P, 512], F32, name="mps_t", tag="tp")
+            else:
+                mps = psa.tile([P, 512], F32, name="mps_a", tag="sa")
             for g in range(2):
                 w, wsc = cw(g, m, 0)
                 nc.tensor.matmul_mx(
@@ -345,27 +366,29 @@ def tile_seteq3to3_t_kernel(tc, x, coefs, bias, out):
                     nc.gpsimd.tensor_tensor(out=b[:].rearrange("p (i j k) -> p i j k", i=8, j=8), in0=p0b, in1=p1b, op=ADD)
                     pre[(n, m)] = b
 
-        def finish(fin, n):
-            osb = fin.tile([P, 2, 512], F32, name="osb")
-            for m in range(2):
+        def finish(fin, ns):
+            halves = [(n, m) for n in ns for m in range(2)]
+            osb = {n: fin.tile([P, 2, 512], F32, name="osb") for n in ns}
+            for n, m in halves:
                 if (n, m) in pre:
-                    nc.vector.tensor_tensor(out=osb[:, m], in0=mains[(n, m)][:], in1=pre[(n, m)][:], op=ADD)
+                    nc.vector.tensor_tensor(out=osb[n][:, m], in0=mains[(n, m)][:], in1=pre[(n, m)][:], op=ADD)
                 else:
                     nc.vector.tensor_tensor(
-                        out=osb[:, m].rearrange("p (i j k) -> p i j k", i=8, j=8),
+                        out=osb[n][:, m].rearrange("p (i j k) -> p i j k", i=8, j=8),
                         in0=mains[(n, m)][:].rearrange("p (i j k) -> p i j k", i=8, j=8), in1=spread(n, m)[0], op=ADD,
                     )
-            for m in range(2):
-                if (n, m) not in pre:
-                    o = osb[:, m].rearrange("p (i j k) -> p i j k", i=8, j=8)
-                    nc.vector.tensor_tensor(out=o, in0=o, in1=spread(n, m)[1], op=ADD)
-            for m in range(2):
-                o = osb[:, m].rearrange("p (e k) -> p e k", k=8)
+            rest = [h for h in halves if h not in pre]
+            for n, m in rest:
+                o = osb[n][:, m].rearrange("p (i j k) -> p i j k", i=8, j=8)
+                nc.vector.tensor_tensor(out=o, in0=o, in1=spread(n, m)[1], op=ADD)
+            order = [h for h in halves if h in pre] + rest
+            for i, (n, m) in enumerate(order):
+                o = osb[n][:, m].rearrange("p (e k) -> p e k", k=8)
                 nc.vector.tensor_tensor(out=o, in0=o, in1=spread(n, m)[2], op=ADD)
                 if n == NBATCH - 1:
-                    nc.sync.dma_start(out=o_v[n][:, m], in_=osb[:, m])
-            if n < NBATCH - 1:
-                nc.sync.dma_start(out=o_v[n], in_=osb[:])
+                    nc.sync.dma_start(out=o_v[n][:, m], in_=osb[n][:, m])
+                elif (n, 1 - m) in order[0:i]:
+                    nc.sync.dma_start(out=o_v[n], in_=osb[n][:])
 
         load(0)
         bz = keep.tile([P, P], BF16, name="bz")
@@ -400,8 +423,12 @@ def tile_seteq3to3_t_kernel(tc, x, coefs, bias, out):
 
         state = {"cgr": [], "ready": [], "half": None, "whole": None}
 
-        def open_group(grp, fin):
+        def open_group(grp, m, fin):
+            sum_over_i(m)
             fold(grp)
+            quantise_x(m)
+            fold_end(grp)
+            sum_over_i_end(m)
             n0, gn = GROUPS[grp]
             for n in range(n0, n0 + gn):
                 prepare(fin, n)
@@ -421,21 +448,22 @@ def tile_seteq3to3_t_kernel(tc, x, coefs, bias, out):
                 p_products(late, behind, 1)
                 regroup(n, "s", (1,))
                 p2_out(behind, 1)
-                open_group(behind, fin)
+                open_group(behind, m, fin)
             if state["whole"] is not None:
-                open_group(state["whole"], fin)
+                open_group(state["whole"], m, fin)
                 state["whole"] = None
             now = state["ready"][0:2]
             state["ready"] = state["ready"][2:]
             todo = [(nb, mb) for nb in now for mb in range(2)]
-            for nb, mb in todo[0:1]:
+            start = 0 if behind is not None else 1
+            for nb, mb in todo[0:start]:
                 main_product(nb, mb)
             transposes(n, 0)
             transposes(n, 1)
             if behind is None:
                 regroup(n, "s", (0,))
             sums(m, 0)
-            for nb, mb in todo[1:2]:
+            for nb, mb in todo[start:2]:
                 main_product(nb, mb)
             transposes(n, 2)
             transposes(n, 3)
@@ -450,10 +478,13 @@ def tile_seteq3to3_t_kernel(tc, x, coefs, bias, out):
                 sums(n, 0)
                 sums(n, 1)
             sum_over_i(m)
+            quantise_x(m)
+            sum_over_i_end(m)
             regroup(n, "v", (0, 1))
             if n == 0:
                 sum_over_i(n)
-            quantise_x(m)
+                quantise_x(n)
+                sum_over_i_end(n)
             if state["cgr"]:
                 coef_quantise(k - 1, state["cgr"])
                 state["cgr"] = []
@@ -461,9 +492,7 @@ def tile_seteq3to3_t_kernel(tc, x, coefs, bias, out):
                 state["cgr"] = coef_regroup(cst, k)
                 cload(cst, k + 2)
             for nb in now:
-                finish(fin, nb)
-            if last:
-                sum_over_i(n)
+                finish(fin, [nb])
             if k in quant_at:
                 group_quantise(late, quant_at[k])
             if last:

@@ -103,8 +103,8 @@ def tile_seteq3to3_t_kernel(tc, x, coefs, bias, out):
                 if who != ("v" if n < 1 or (n < XV and g == 1) else "s"):
                     continue
                 xg = xgp.tile([P, 2048], BF16, align_bytes=64, name="xg%d" % g)
-                dst = xg[:].rearrange("p (c i t) -> p c t i", i=4, t=4)
-                src = raws[n][:, g * 2048 : (g + 1) * 2048].rearrange("p (t c i) -> p c t i", t=4, i=4)
+                dst = xg[:].rearrange("p (c i t) -> p c t i", i=8, t=4)
+                src = raws[n][:, g * 2048 : (g + 1) * 2048].rearrange("p (t c i) -> p c t i", t=4, i=8)
                 if who == "v":
                     nc.vector.tensor_copy(out=dst, in_=src)
                 else:

@@ -208,7 +208,11 @@ def tile_seteq3to3_t_kernel(tc, x, coefs, bias, out):
             if step < 4:
                 m, g = divmod(step, 2)
                 craw = cst.tile([P, 4, 128 * NB], BF16, name="craw")
-                nc.sync.dma_start(out=craw[:], in_=c_v[g][:, :, m * 128 * NB : (m + 1) * 128 * NB])
+                pieces = 2 if step == 0 else 1
+                w = 128 * NB // pieces
+                for i in range(pieces):
+                    o = m * 128 * NB + i * w
+                    nc.sync.dma_start(out=craw[:, :, i * w : (i + 1) * w], in_=c_v[g][:, :, o : o + w])
                 craws[step] = craw
 
         def coef_regroup(cst, step):
@@ -217,10 +221,11 @@ def tile_seteq3to3_t_kernel(tc, x, coefs, bias, out):
             for b0, b1, who in CHUNKS:
                 cgr = cst.tile([P, 2048], BF16, align_bytes=64, name="cgr", bufs=6)
                 dst = cgr[:, 0 : (b1 - b0) * 512].rearrange("p (b s t) -> p s t b", b=b1 - b0, t=4)
-                if who[0] == "s":
-                    nc.scalar.copy(out=dst, in_=src[:, :, :, b0:b1])
-                else:
-                    nc.vector.tensor_copy(out=dst, in_=src[:, :, :, b0:b1])
+                for s0, s1 in ((0, 64), (64, 128)) if step == 0 and who == "s" else ((0, 128),):
+                    if who[0] == "s":
+                        nc.scalar.copy(out=dst[:, s0:s1], in_=src[:, s0:s1, :, b0:b1])
+                    else:
+                        nc.vector.tensor_copy(out=dst[:, s0:s1], in_=src[:, s0:s1, :, b0:b1])
                 tiles.append(cgr)
             return tiles
 
@@ -417,7 +422,7 @@ def tile_seteq3to3_t_kernel(tc, x, coefs, bias, out):
         bias_sb = keep.tile([P, 2], F32, name="bias_sb")
 
         def bias_setup():
-            bps = pst.tile([P, 1024], BF16, name="bps", tag="tp")
+            bps = psx.tile([P, 1024], BF16, name="bps", tag="mx")
             nc.tensor.transpose(bps[:, 0:P], bz[:], ident[:])
             nc.scalar.copy(out=bias_sb[:], in_=bps[:, 0:2])
 
@@ -455,7 +460,7 @@ def tile_seteq3to3_t_kernel(tc, x, coefs, bias, out):
             now = state["ready"][0:2]
             state["ready"] = state["ready"][2:]
             todo = [(nb, mb) for nb in now for mb in range(2)]
-            start = 0 if behind is not None else 1
+            start = 0
             for nb, mb in todo[0:start]:
                 main_product(nb, mb)
             transposes(n, 0)

from contextlib import ExitStack

import concourse.mybir as mybir
from concourse.masks import make_identity

F32 = mybir.dt.float32
BF16 = mybir.dt.bfloat16
U32 = mybir.dt.uint32
U8 = mybir.dt.uint8
FP8X4 = mybir.dt.float8_e4m3fn_x4
ADD = mybir.AluOpType.add
AX = mybir.AxisListType.X
AXY = mybir.AxisListType.XY
IDENT = mybir.ActivationFunctionType.Identity

P = 128
NBATCH = 16
GROUPS = ((0, 4), (4, 4), (8, 4), (12, 2), (14, 2))
NB = 19
CHUNKS = ((0, 4, "s"), (4, 8, "w"), (8, 12, "s2"), (12, 16, "v"), (16, 19, "u"))
XV = 5
LATE_MAIN = 12
PE_A0 = (3, 15)
FLOPS = 2 * 1024 * 256 * (8192 + 9 * 1024 + 9 * 128)


def tile_seteq3to3_t_kernel(tc, x, coefs, bias, out):
    nc = tc.nc
    x_v = x.rearrange("n (g p t) i j k -> n p g (t i j k)", g=2, p=P, t=4)
    c_v = coefs.rearrange("(g p t) s b -> g p t (s b)", g=2, p=P, t=4)
    o_v = out.rearrange("n (m p) i j k -> n p m (i j k)", m=2, p=P)
    b_v = bias.rearrange("o (m p) a b c -> (o m) (p a b c)", m=2, p=P)

    with ExitStack() as ctx:
        ctx.enter_context(tc.manual_schedule())
        keep = ctx.enter_context(tc.tile_pool(name="keep", bufs=1))
        xin = ctx.enter_context(tc.tile_pool(name="xin", bufs=3))
        xtp = ctx.enter_context(tc.tile_pool(name="xtp", bufs=2))
        xgp = ctx.enter_context(tc.tile_pool(name="xgp", bufs=2))
        xcd = ctx.enter_context(tc.tile_pool(name="xcd", bufs=6))
        s1p = ctx.enter_context(tc.tile_pool(name="s1p", bufs=1))
        agp = ctx.enter_context(tc.tile_pool(name="agp", bufs=2))
        pst = ctx.enter_context(tc.psum_pool(name="pst", bufs=2))
        psa = ctx.enter_context(tc.psum_pool(name="psa", bufs=2))
        psx = ctx.enter_context(tc.psum_pool(name="psx", bufs=4))

        cq = keep.tile([P, 4 * NB * P], U32, align_bytes=64, name="cq")
        cs = keep.tile([P, 4 * NB * P], U8, align_bytes=64, name="cs")

        group_of = {}
        stage_at = {}
        quant_at = {}
        for gi, (n0, gn) in enumerate(GROUPS):
            for n in range(n0, n0 + gn):
                group_of[n] = gi
            done = n0 + gn - (1 if gi == len(GROUPS) - 1 else 0)
            quant_at[done] = gi
            stage_at[done + 1] = gi

        made = set()
        raws = {}
        craws = {}
        xgs = {}
        xts = {}
        sas = {}
        a0s = {}
        agrs = {}
        xqs = {}
        gcodes = {}
        psbs = {}
        qsbs = {}
        pss = {}
        mains = {}
        pre = {}
        r2s = {}

        def live(n):
            return 0 <= n < NBATCH

        def load(n):
            if live(n):
                raw = xin.tile([P, 4096], BF16, name="raw")
                if n == 0:
                    for g in range(2):
                        nc.sync.dma_start(out=raw[:, g * 2048 : (g + 1) * 2048], in_=x_v[n][:, g])
                else:
                    nc.sync.dma_start(out=raw[:].rearrange("p (g w) -> p g w", g=2), in_=x_v[n])
                raws[n] = raw

        def agr_view(n):
            grp = group_of[n]
            n0, gn = GROUPS[grp]
            if grp not in agrs:
                agrs[grp] = agp.tile([P, 3, 2048], BF16, align_bytes=64, name="agr")
            return agrs[grp][:, :, 0 : gn * 512].rearrange("p a (g n q t) -> p a g n q t", g=2, n=gn, t=4), n - n0

        def regroup(n, who, halves):
            if not live(n):
                return
            if n not in xgs:
                xgs[n] = []
            for g in halves:
                if who != ("v" if n < 1 or (n < XV and g == 1) else "s"):
                    continue
                xg = xgp.tile([P, 2048], BF16, align_bytes=64, name="xg%d" % g)
                dst = xg[:].rearrange("p (c i t) -> p c t i", i=8, t=4)
                src = raws[n][:, g * 2048 : (g + 1) * 2048].rearrange("p (t c i) -> p c t i", t=4, i=8)
                if who == "v":
                    nc.vector.tensor_copy(out=dst, in_=src)
                else:
                    nc.scalar.copy(out=dst, in_=src)
                xgs[n].append(xg)

        def transposes(n, u):
            if not live(n):
                return
            if u == 0:
                xts[n] = xtp.tile([P, 4096], BF16, name="xT")
            tp = pst.tile([P, 1024], BF16, name="tp")
            for r in range(8):
                o = (u * 8 + r) * P
                nc.tensor.transpose(tp[:, r * P : (r + 1) * P], raws[n][:, o : o + P], ident[:])
            nc.scalar.copy(out=xts[n][:, u * 1024 : (u + 1) * 1024], in_=tp[:])

        def sums(n, g):
            if not live(n) or (n, g) in made:
                return
            made.add((n, g))
            sas[(n, g)] = psa.tile([P, 512], F32, name="sa")
            if n in PE_A0 and g == 0:
                a0s[n] = pst.tile([P, 1024], BF16, name="a0", tag="tp")[:].bitcast(F32) if n == NBATCH - 1 else psx.tile([P, 512], F32, name="a0", tag="mx")[:]
            sa = sas[(n, g)][:, 0:288].bitcast(BF16)
            sv = sas[(n, g)][:, 288:352]
            for t in range(4):
                with nc.allow_low_precision(reason="each sum is made whole in float32 by one matmul and rounded once to bfloat16"):
                    for c in range(4):
                        o = ((g * 4 + t) * 4 + c) * P
                        nc.tensor.matmul(
                            out=sa[:, (t * 4 + c) * 36 : (t * 4 + c) * 36 + 34],
                            lhsT=xts[n][:, o : o + P], rhs=sb[:, 0:34], start=True, stop=True,
                        )
                for c in range(4):
                    o = ((g * 4 + t) * 4 + c) * P
                    nc.tensor.matmul(
                        out=sv[:, t * 16 : (t + 1) * 16],
                        lhsT=xts[n][:, o : o + P], rhs=sb[:, 34:50], start=(c == 0), stop=(c == 3),
                    )
                if n in PE_A0:
                    for c in range(4):
                        o = ((g * 4 + t) * 4 + c) * P
                        nc.tensor.matmul(
                            out=a0s[n][:, (g * 4 + t) * 64 : (g * 4 + t + 1) * 64],
                            lhsT=xts[n][:, o : o + P], rhs=sb[:, 64:128], start=(c == 0), stop=(c == 3),
                        )
            agr_v, ni = agr_view(n)
            sa_v = sas[(n, g)][:, 0:288].bitcast(BF16).rearrange("p (t c w) -> p t c w", t=4, c=4)
            nc.scalar.copy(
                out=agr_v[:, 1:3, g, ni].rearrange("p a (c e) t -> p a c e t", c=4),
                in_=sa_v[:, :, :, 0:32].rearrange("p t c (a e) -> p a c e t", a=2),
            )
            cols = slice(ni * 8, (ni + 1) * 8)
            nc.scalar.copy(
                out=vgr_v[:, 2, g, cols, :].rearrange("p (c i) t -> p c i t", c=4),
                in_=sa_v[:, :, :, 32:34].rearrange("p t c i -> p c i t"),
            )
            nc.scalar.copy(out=vgr_v[:, 0:2, g, cols, :], in_=sas[(n, g)][:, 288:352].rearrange("p (t v r) -> p v r t", t=4, v=2))
            if n in PE_A0:
                nc.scalar.copy(
                    out=agr_v[:, 0, g, ni], in_=a0s[n][:, g * 256 : (g + 1) * 256].rearrange("p (t q) -> p q t", t=4)
                )

        def sum_over_i(n):
            if not live(n) or n in PE_A0 or ("i", n) in made:
                return
            made.add(("i", n))
            r1 = s1p.tile([P, 2, 1024], F32, name="r1")
            r2 = s1p.tile([P, 2, 512], F32, name="r2")
            for g in range(2):
                nc.vector.tensor_tensor(out=r1[:, g], in0=xgs[n][g][:, 0:1024], in1=xgs[n][g][:, 1024:2048], op=ADD)
            for g in range(2):
                nc.vector.tensor_tensor(out=r2[:, g], in0=r1[:, g, 0:512], in1=r1[:, g, 512:1024], op=ADD)
            r2s[n] = r2

        def sum_over_i_end(n):
            if n not in r2s or ("e", n) in made:
                return
            made.add(("e", n))
            agr_v, ni = agr_view(n)
            r2 = r2s[n]
            with nc.allow_low_precision(reason="the sum is made in float32 and rounded once to bfloat16"):
                nc.vector.tensor_tensor(
                    out=agr_v[:, 0, :, ni].rearrange("p g q t -> p g (q t)"), in0=r2[:, :, 0:256], in1=r2[:, :, 256:512], op=ADD,
                )

        def quantise_x(n):
            if not live(n) or ("q", n) in made:
                return
            made.add(("q", n))
            xq = xcd.tile([P, 1024], U32, align_bytes=64, name="xq")
            xs = xcd.tile([P, 1024], U8, align_bytes=64, name="xs")
            for g in range(2):
                nc.vector.quantize_mx(
                    out=xq[:, g * 512 : (g + 1) * 512].bitcast(FP8X4), scales=xs[:, g * 512 : (g + 1) * 512], in_=xgs[n][g][:]
                )
            xqs[n] = (xq, xs)

        def cload(cst, step):
            if step < 4:
                m, g = divmod(step, 2)
                craw = cst.tile([P, 4, 128 * NB], BF16, name="craw")
                pieces = 2 if step == 0 else 1
                w = 128 * NB // pieces
                for i in range(pieces):
                    o = m * 128 * NB + i * w
                    nc.sync.dma_start(out=craw[:, :, i * w : (i + 1) * w], in_=c_v[g][:, :, o : o + w])
                craws[step] = craw

        def coef_regroup(cst, step):
            src = craws[step][:].rearrange("p t (s b) -> p s t b", b=NB)
            tiles = []
            for b0, b1, who in CHUNKS:
                cgr = cst.tile([P, 2048], BF16, align_bytes=64, name="cgr", bufs=6)
                dst = cgr[:, 0 : (b1 - b0) * 512].rearrange("p (b s t) -> p s t b", b=b1 - b0, t=4)
                for s0, s1 in ((0, 64), (64, 128)) if step == 0 and who == "s" else ((0, 128),):
                    if who[0] == "s":
                        nc.scalar.copy(out=dst[:, s0:s1], in_=src[:, s0:s1, :, b0:b1])
                    else:
                        nc.vector.tensor_copy(out=dst[:, s0:s1], in_=src[:, s0:s1, :, b0:b1])
                tiles.append(cgr)
            return tiles

        def coef_quantise(step, tiles):
            m, g = divmod(step, 2)
            base = (g * 2 + m) * NB * P
            for (b0, b1, who), cgr in sorted(zip(CHUNKS, tiles), key=lambda z: z[0][2][0] == "s"):
                pieces = ((0, 4),) if b1 - b0 == 4 else ((0, 2), (2, 3))
                for q0, q1 in pieces:
                    nc.vector.quantize_mx(
                        out=cq[:, base + (b0 + q0) * P : base + (b0 + q1) * P].bitcast(FP8X4),
                        scales=cs[:, base + (b0 + q0) * P : base + (b0 + q1) * P],
                        in_=cgr[:, q0 * 512 : q1 * 512],
                    )

        def cw(g, m, b):
            o = ((g * 2 + m) * NB + b) * P
            return cq[:, o : o + P].bitcast(FP8X4), cs[:, o : o + P]

        def group_quantise(late, grp):
            gn = GROUPS[grp][1]
            agr = agrs[grp]
            aq = late.tile([P, 1536], U32, align_bytes=64, name="aq")
            asc = late.tile([P, 1536], U8, align_bytes=64, name="asc")
            vq = late.tile([P, 512], U32, align_bytes=64, name="vq")
            vs = late.tile([P, 512], U8, align_bytes=64, name="vs")
            nc.vector.quantize_mx(out=vq[:].bitcast(FP8X4), scales=vs[:], in_=vgr[:])
            for a3 in range(3):
                nc.vector.quantize_mx(
                    out=aq[:, a3 * 512 : a3 * 512 + gn * 128].bitcast(FP8X4),
                    scales=asc[:, a3 * 512 : a3 * 512 + gn * 128],
                    in_=agr[:, a3, 0 : gn * 512],
                )
            gcodes[grp] = (aq, asc, vq, vs)

        def a_group(acc, grp, m, pl):
            aq, asc, vq, vs = gcodes[grp]
            nw = GROUPS[grp][1] * 64
            for idx in range(6):
                a3, g = divmod(idx, 2)
                w, wsc = cw(g, m, 1 + 3 * a3 + pl)
                o = a3 * 512 + g * nw
                nc.tensor.matmul_mx(
                    out=acc, lhsT=w, lhsT_scale=wsc,
                    rhs=aq[:, o : o + nw].bitcast(FP8X4), rhs_scale=asc[:, o : o + nw],
                    start=(idx == 0), stop=(idx == 5),
                )

        def q_products(late, grp):
            gn = GROUPS[grp][1]
            aq, asc, vq, vs = gcodes[grp]
            for m in range(2):
                qsb = late.tile([P, 3, 32], F32, name="qsb%d" % m)
                qps = psx.tile([P, 512], F32, name="qps", tag="mx")
                for pl in range(3):
                    for idx in range(6):
                        a3, g = divmod(idx, 2)
                        w, wsc = cw(g, m, 10 + 3 * a3 + pl)
                        o = (a3 * 2 + g) * 64
                        nc.tensor.matmul_mx(
                            out=qps[:, pl * P : (pl + 1) * P], lhsT=w, lhsT_scale=wsc,
                            rhs=vq[:, o : o + P].bitcast(FP8X4), rhs_scale=vs[:, o : o + P],
                            start=(idx == 0), stop=(idx == 5),
                        )
                nc.scalar.copy(
                    out=qsb[:, :, 0 : gn * 8], in_=qps[:, 0:384].rearrange("p (l c) -> p l c", l=3)[:, :, 0 : gn * 8]
                )
                qsbs[(grp, m)] = qsb

        def p_products(late, grp, m):
            nw = GROUPS[grp][1] * 64
            p10 = late.tile([P, 2, 256], F32, name="p10_%d" % m)
            p2 = late.tile([P, 256], F32, name="p2_%d" % m)
            pps = psx.tile([P, 512], F32, name="pps", tag="mx")
            a_group(pps[:, 0:nw], grp, m, 1)
            a_group(pps[:, 256 : 256 + nw], grp, m, 0)
            pp2 = psx.tile([P, 512], F32, name="pp2", tag="mx")
            a_group(pp2[:, 0:nw], grp, m, 2)
            psbs[(grp, m)] = (p10, p2)
            pss[(grp, m)] = (pps, pp2)

        def p2_out(grp, m):
            nw = GROUPS[grp][1] * 64
            nc.scalar.activation(
                out=psbs[(grp, m)][1][:, 0:nw], in_=pss[(grp, m)][1][:, 0:nw], func=IDENT, bias=bias_sb[:, m : m + 1]
            )

        def fold(grp):
            gn = GROUPS[grp][1]
            nw = gn * 64
            for m in range(2):
                nc.vector.tensor_tensor(
                    out=psbs[(grp, m)][0][:, :, 0:nw].rearrange("p l (e k) -> p l e k", k=8),
                    in0=pss[(grp, m)][0][:].rearrange("p (l c) -> p l c", l=2)[:, :, 0:nw].rearrange("p l (e k) -> p l e k", k=8),
                    in1=qsbs[(grp, m)][:, 0:2, 0 : gn * 8].unsqueeze(3).to_broadcast([P, 2, gn * 8, 8]),
                    op=ADD,
                )

        def fold_end(grp):
            gn = GROUPS[grp][1]
            nw = gn * 64
            for m in range(2):
                p0 = psbs[(grp, m)][0][:, 1, 0:nw].rearrange("p (n j k) -> p n j k", n=gn, k=8)
                nc.vector.tensor_tensor(
                    out=p0, in0=p0,
                    in1=qsbs[(grp, m)][:, 2, 0 : gn * 8].rearrange("p (n k) -> p n k", n=gn).unsqueeze(2).to_broadcast([P, gn, 8, 8]),
                    op=ADD,
                )

        def spread(n, m):
            grp = group_of[n]
            ni = n - GROUPS[grp][0]
            p10, p2 = psbs[(grp, m)]
            sl = slice(ni * 64, (ni + 1) * 64)
            p0b = p10[:, 1, sl].rearrange("p (j k) -> p j k", j=8).unsqueeze(1).to_broadcast([P, 8, 8, 8])
            p1b = p10[:, 0, sl].rearrange("p (i k) -> p i k", i=8).unsqueeze(2).to_broadcast([P, 8, 8, 8])
            p2b = p2[:, sl].unsqueeze(2).to_broadcast([P, 64, 8])
            return p0b, p1b, p2b

        def main_product(n, m):
            xq, xs = xqs[n]
            if n < LATE_MAIN:
                mps = psx.tile([P, 512], F32, name="mps", tag="mx")
            elif n % 2 == 0:
                mps = pst.tile([P, 512], F32, name="mps_t", tag="tp")
            else:
                mps = psa.tile([P, 512], F32, name="mps_a", tag="sa")
            for g in range(2):
                w, wsc = cw(g, m, 0)
                nc.tensor.matmul_mx(
                    out=mps[:], lhsT=w, lhsT_scale=wsc,
                    rhs=xq[:, g * 512 : (g + 1) * 512].bitcast(FP8X4), rhs_scale=xs[:, g * 512 : (g + 1) * 512],
                    start=(g == 0), stop=(g == 1),
                )
            mains[(n, m)] = mps

        def prepare(fin, n):
            n0, gn = GROUPS[group_of[n]]
            for m in range(2):
                if 2 * (n - n0) + m > gn:
                    b = fin.tile([P, 512], F32, name="b")
                    p0b, p1b, p2b = spread(n, m)
                    nc.gpsimd.tensor_tensor(out=b[:].rearrange("p (i j k) -> p i j k", i=8, j=8), in0=p0b, in1=p1b, op=ADD)
                    pre[(n, m)] = b

        def finish(fin, ns):
            halves = [(n, m) for n in ns for m in range(2)]
            osb = {n: fin.tile([P, 2, 512], F32, name="osb") for n in ns}
            for n, m in halves:
                if (n, m) in pre:
                    nc.vector.tensor_tensor(out=osb[n][:, m], in0=mains[(n, m)][:], in1=pre[(n, m)][:], op=ADD)
                else:
                    nc.vector.tensor_tensor(
                        out=osb[n][:, m].rearrange("p (i j k) -> p i j k", i=8, j=8),
                        in0=mains[(n, m)][:].rearrange("p (i j k) -> p i j k", i=8, j=8), in1=spread(n, m)[0], op=ADD,
                    )
            rest = [h for h in halves if h not in pre]
            for n, m in rest:
                o = osb[n][:, m].rearrange("p (i j k) -> p i j k", i=8, j=8)
                nc.vector.tensor_tensor(out=o, in0=o, in1=spread(n, m)[1], op=ADD)
            order = [h for h in halves if h in pre] + rest
            for i, (n, m) in enumerate(order):
                o = osb[n][:, m].rearrange("p (e k) -> p e k", k=8)
                nc.vector.tensor_tensor(out=o, in0=o, in1=spread(n, m)[2], op=ADD)
                if n == NBATCH - 1:
                    nc.sync.dma_start(out=o_v[n][:, m], in_=osb[n][:, m])
                elif (n, 1 - m) in order[0:i]:
                    nc.sync.dma_start(out=o_v[n], in_=osb[n][:])

        load(0)
        bz = keep.tile([P, P], BF16, name="bz")
        nc.vector.memset(bz[:], 0.0)
        nc.sync.dma_start(out=bz[0:2, :], in_=b_v)
        ident = keep.tile([P, P], BF16, name="ident")
        make_identity(nc, ident[:])
        sf = keep.tile([P, P], F32, name="sf")
        nc.vector.memset(sf[:], 0.0)
        nc.vector.tensor_reduce(
            out=sf[:, 0:16].rearrange("p (i k) -> p i k", i=2),
            in_=ident[:].rearrange("p (i j k) -> p i k j", i=2, j=8), axis=AX, op=ADD,
        )
        nc.vector.tensor_reduce(out=sf[:, 16:32], in_=ident[:].rearrange("p (e k) -> p e k", k=8), axis=AX, op=ADD)
        nc.vector.tensor_reduce(out=sf[:, 32:34], in_=ident[:].rearrange("p (i e) -> p i e", i=2), axis=AX, op=ADD)
        nc.vector.tensor_reduce(out=sf[:, 34:42], in_=ident[:].rearrange("p (e k) -> p k e", k=8), axis=AX, op=ADD)
        nc.vector.tensor_reduce(
            out=sf[:, 42:50], in_=ident[:].rearrange("p (i j k) -> p j i k", i=2, j=8), axis=AXY, op=ADD
        )
        nc.vector.tensor_reduce(out=sf[:, 64:128], in_=ident[:].rearrange("p (i e) -> p e i", i=2), axis=AX, op=ADD)
        sb = keep.tile([P, P], BF16, name="sb")
        nc.vector.tensor_copy(out=sb[:], in_=sf[:])
        vgr = keep.tile([P, 2048], BF16, align_bytes=64, name="vgr")
        nc.vector.memset(vgr[:], 0.0)
        vgr_v = vgr[:, 0:1536].rearrange("p (v g c t) -> p v g c t", v=3, g=2, t=4)
        bias_sb = keep.tile([P, 2], F32, name="bias_sb")

        def bias_setup():
            bps = psx.tile([P, 1024], BF16, name="bps", tag="mx")
            nc.tensor.transpose(bps[:, 0:P], bz[:], ident[:])
            nc.scalar.copy(out=bias_sb[:], in_=bps[:, 0:2])

        state = {"cgr": [], "ready": [], "half": None, "whole": None}

        def open_group(grp, m, fin):
            sum_over_i(m)
            fold(grp)
            quantise_x(m)
            fold_end(grp)
            sum_over_i_end(m)
            n0, gn = GROUPS[grp]
            for n in range(n0, n0 + gn):
                prepare(fin, n)
            state["ready"] = state["ready"] + list(range(n0, n0 + gn))

        def step(k, cst, late, fin):
            n = k
            m = k - 1
            last = n == NBATCH - 1
            load(k + 2)
            grp = stage_at.get(k)
            behind = state["half"]
            state["half"] = None
            if behind is not None:
                regroup(n, "s", (0,))
                p2_out(behind, 0)
                p_products(late, behind, 1)
                regroup(n, "s", (1,))
                p2_out(behind, 1)
                open_group(behind, m, fin)
            if state["whole"] is not None:
                open_group(state["whole"], m, fin)
                state["whole"] = None
            now = state["ready"][0:2]
            state["ready"] = state["ready"][2:]
            todo = [(nb, mb) for nb in now for mb in range(2)]
            start = 0
            for nb, mb in todo[0:start]:
                main_product(nb, mb)
            transposes(n, 0)
            transposes(n, 1)
            if behind is None:
                regroup(n, "s", (0,))
            sums(m, 0)
            for nb, mb in todo[start:2]:
                main_product(nb, mb)
            transposes(n, 2)
            transposes(n, 3)
            if behind is None and (grp is None or last):
                regroup(n, "s", (1,))
            sums(m, 1)
            for nb, mb in todo[2:]:
                main_product(nb, mb)
            if grp is not None and not last:
                regroup(n, "s", (1,))
            if last:
                sums(n, 0)
                sums(n, 1)
            sum_over_i(m)
            quantise_x(m)
            sum_over_i_end(m)
            regroup(n, "v", (0, 1))
            if n == 0:
                sum_over_i(n)
                quantise_x(n)
                sum_over_i_end(n)
            if state["cgr"]:
                coef_quantise(k - 1, state["cgr"])
                state["cgr"] = []
            if k < 4:
                state["cgr"] = coef_regroup(cst, k)
                cload(cst, k + 2)
            for nb in now:
                finish(fin, [nb])
            if k in quant_at:
                group_quantise(late, quant_at[k])
            if last:
                quantise_x(n)
            if grp is not None:
                q_products(late, grp)
                p_products(late, grp, 0)
                if n < NBATCH - 1:
                    state["half"] = grp
                else:
                    p2_out(grp, 0)
                    p_products(late, grp, 1)
                    p2_out(grp, 1)
                    state["whole"] = grp

        with tc.tile_pool(name="cst", bufs=2) as cst:
            cload(cst, 0)
            load(1)
            cload(cst, 1)
            for k in range(4):
                step(k, cst, None, None)
                if k == 0:
                    bias_setup()
            coef_quantise(3, state["cgr"])
            state["cgr"] = []
        late = ctx.enter_context(tc.tile_pool(name="late", bufs=2))
        fin = ctx.enter_context(tc.tile_pool(name="fin", bufs=3))
        for k in range(4, NBATCH + 6):
            step(k, None, late, fin)
